import numpy as np
import ml_dtypes


def mxq(x, axis, fmt="e4m3"):
    dtype, down = {"e4m3": (ml_dtypes.float8_e4m3fn, 7), "e5m2": (ml_dtypes.float8_e5m2, 14)}[fmt]
    v = np.moveaxis(np.asarray(x, np.float32).astype(ml_dtypes.bfloat16).astype(np.float64), axis, -1)
    blocks = v.reshape(v.shape[:-1] + (-1, 32))
    amax = np.abs(blocks).max(-1, keepdims=True)
    byte = np.maximum(np.where(amax > 0, np.frexp(amax)[1] - 1 + 127, 0) - down, 1)
    scale = np.exp2(byte - 127.0)
    codes = (blocks / scale).astype(np.float32).astype(dtype).astype(np.float64)
    return np.moveaxis((codes * scale).reshape(v.shape), -1, axis)


WIDE = False


def mx_kscale(k):
    if not WIDE:
        return np.ones(k)
    levels = np.array([10, -10, 5, -5, 0])
    a = np.random.permutation(np.resize(levels, k // 512 * 4)).reshape(k // 512, 4)
    idx = np.arange(k)
    return np.exp2(a[idx // 512, idx % 128 // 32])


BF16 = ml_dtypes.bfloat16


def bf(x):
    return np.asarray(x, np.float32).astype(BF16)


def f64(x):
    return np.asarray(x).astype(np.float64)


B, N, D = 1, 1024, 1024
P0 = 0.2


def setup_inputs():
    s = mx_kscale(D)
    g = 0.4 + 1.2 * np.random.random_sample((B, 1, N))
    bound = np.sqrt(6.0 / (D + D))
    return {"embedding": bf(np.random.standard_normal((B, D, N)) * g * np.sqrt(P0) / D ** 0.25 * s[None, :, None]),
            "heatm": bf(np.random.standard_normal((B, D, N))),
            "W_b": bf(np.random.uniform(-bound, bound, (D, D)) / s[:, None] / s[None, :])}


def reference(embedding, heatm, W_b):
    eq = mxq(f64(embedding), 1, "e4m3")
    t = np.swapaxes(eq, 1, 2) @ mxq(f64(W_b), 0, "e4m3")
    C = np.tanh(mxq(t, 2, "e4m3") @ eq)
    max_cow = np.max(C, axis=-1, keepdims=True)
    e = np.exp(max_cow - np.max(max_cow, axis=1, keepdims=True))
    return e / np.sum(e, axis=1, keepdims=True)

@@ -1,0 +1,204 @@
+from contextlib import ExitStack
+
+import concourse.mybir as mybir
+from concourse.masks import make_identity
+
+FLOPS = 2 * 2 * 1024 * 1024 * 1024
+BYTES = 2 * 1024 * 1024 * 2 + 1024 * 4
+
+F32 = mybir.dt.float32
+BF16 = mybir.dt.bfloat16
+U32 = mybir.dt.uint32
+U8 = mybir.dt.uint8
+FP8X4 = mybir.dt.float8_e4m3fn_x4
+ACT = mybir.ActivationFunctionType
+ALU = mybir.AluOpType
+AX = mybir.AxisListType
+
+P = 128
+PACK = 4
+G = 2
+PIECE = 256
+NPIECE = 4
+NB = 8
+
+
+def tile_parallelcoattention_kernel(tc, embedding, heatm, W_b, out):
+    nc = tc.nc
+    e_rows = embedding[0].rearrange("(r p) n -> p r n", p=P)
+    w_rows = W_b.rearrange("(r p) n -> p r n", p=P)
+    out_rows = out[0].rearrange("(c q) u -> c (q u)", c=NB)
+
+    with ExitStack() as ctx:
+        keep = ctx.enter_context(tc.tile_pool(name="keep", bufs=1))
+        tpool = ctx.enter_context(tc.tile_pool(name="tpool", bufs=1))
+        psum = ctx.enter_context(tc.psum_pool(name="psum", bufs=4))
+
+        warm = keep.tile([P, 1], F32, name="warm")
+        nc.vector.memset(warm[:], 0.0)
+        warm2 = keep.tile([P, 1], F32, name="warm2")
+        nc.scalar.activation(out=warm2[:], in_=warm[:], func=ACT.Tanh)
+        ident = keep.tile([P, P], F32, name="ident")
+        make_identity(nc, ident[:])
+        ones = keep.tile([P, P], F32, name="ones")
+        nc.vector.memset(ones[:], 1.0)
+        epad = keep.tile([P, P], F32, name="epad")
+        nc.vector.memset(epad[:], 0.0)
+
+        raw = {}
+        grp = {}
+        cod = {}
+        scl = {}
+        order = [("e", 0), ("w", 0), ("w", 1), ("e", 1), ("w", 2), ("w", 3), ("e", 2), ("e", 3)]
+        for key in order:
+            kind, q = key
+            src = e_rows if kind == "e" else w_rows
+            raw[key] = keep.tile([P, G * PACK, PIECE], BF16, name="raw_%s%d" % key)
+            nc.sync.dma_start(out=raw[key][:], in_=src[:, :, q * PIECE:(q + 1) * PIECE])
+            grp[key] = keep.tile([P, G, PIECE, PACK], BF16, name="grp_%s%d" % key, align_bytes=64)
+            cod[key] = keep.tile([P, G, PIECE], U32, name="cod_%s%d" % key, align_bytes=64)
+            scl[key] = keep.tile([P, G, PIECE], U8, name="scl_%s%d" % key, align_bytes=64)
+
+        def regroup(key, g, eng):
+            src = raw[key][:, g * PACK:(g + 1) * PACK, :].rearrange("p t (c i) -> p c t i", i=4)
+            dst = grp[key][:, g].rearrange("p (c i) t -> p c t i", i=4)
+            if eng == "v":
+                nc.vector.tensor_copy(out=dst, in_=src)
+            else:
+                nc.scalar.copy(out=dst, in_=src)
+
+        def quantise(key, g):
+            nc.vector.quantize_mx(
+                out=cod[key][:, g, :].bitcast(FP8X4),
+                scales=scl[key][:, g, :],
+                in_=grp[key][:, g].rearrange("p n t -> p (n t)"),
+            )
+
+        def prepare(key):
+            regroup(key, 0, "v")
+            regroup(key, 1, "s")
+            quantise(key, 0)
+            quantise(key, 1)
+
+        tgr = {}
+        tcod = {}
+        tscl = {}
+
+        def mm1(g2, b):
+            pt = psum.tile([P, PACK, P], F32, name="pt", tag="t")
+            ek = ("e", b // 2)
+            ecol = slice((b % 2) * P, (b % 2) * P + P)
+            for j in range(PACK):
+                wk = ("w", 2 * g2 + j // 2)
+                wcol = slice((j % 2) * P, (j % 2) * P + P)
+                for g1 in range(G):
+                    nc.tensor.matmul_mx(
+                        out=pt[:, j, :],
+                        lhsT=cod[wk][:, g1, wcol].bitcast(FP8X4),
+                        lhsT_scale=scl[wk][:, g1, wcol],
+                        rhs=cod[ek][:, g1, ecol].bitcast(FP8X4),
+                        rhs_scale=scl[ek][:, g1, ecol],
+                        start=(g1 == 0),
+                        stop=(g1 == G - 1),
+                    )
+            if b not in tgr:
+                tgr[b] = tpool.tile([P, G, P, PACK], BF16, name="tgr%d" % b, align_bytes=64)
+            nc.scalar.copy(out=tgr[b][:, g2], in_=pt[:].rearrange("p j n -> p n j"))
+
+        def quantise_t(b):
+            tcod[b] = tpool.tile([P, G, P], U32, name="tcod%d" % b, align_bytes=64)
+            tscl[b] = tpool.tile([P, G, P], U8, name="tscl%d" % b, align_bytes=64)
+            nc.vector.quantize_mx(
+                out=tcod[b][:].rearrange("p g n -> p (g n)").bitcast(FP8X4),
+                scales=tscl[b][:].rearrange("p g n -> p (g n)"),
+                in_=tgr[b][:].rearrange("p g n t -> p (g n t)"),
+            )
+
+        mx16 = keep.tile([P, 2 * NB], F32, name="mx16")
+
+        def mm2(b, h):
+            pc = psum.tile([P, 2, PIECE], F32, name="pc", tag="c")
+            for s in range(2):
+                ek = ("e", 2 * h + s)
+                for g2 in range(G):
+                    nc.tensor.matmul_mx(
+                        out=pc[:, s, :],
+                        lhsT=tcod[b][:, g2, :].bitcast(FP8X4),
+                        lhsT_scale=tscl[b][:, g2, :],
+                        rhs=cod[ek][:, g2, :].bitcast(FP8X4),
+                        rhs_scale=scl[ek][:, g2, :],
+                        start=(g2 == 0),
+                        stop=(g2 == G - 1),
+                    )
+            nc.vector.reduce_max(
+                out=mx16[:, 2 * b + h:2 * b + h + 1],
+                in_=pc[:].rearrange("p s m -> p (s m)"),
+                axis=AX.X,
+            )
+
+        prepare(("e", 0))
+        prepare(("w", 0))
+        prepare(("w", 1))
+        mm1(0, 0)
+        mm1(0, 1)
+        prepare(("e", 1))
+        mm1(0, 2)
+        mm1(0, 3)
+        prepare(("w", 2))
+        prepare(("w", 3))
+        for b in range(4):
+            mm1(1, b)
+            quantise_t(b)
+        prepare(("e", 2))
+        for b in range(4):
+            mm2(b, 0)
+        for b in (4, 5):
+            mm1(0, b)
+            mm1(1, b)
+            quantise_t(b)
+        prepare(("e", 3))
+        mm2(4, 0)
+        mm2(5, 0)
+        mm1(0, 6)
+        mm1(1, 6)
+        quantise_t(6)
+        mm2(0, 1)
+        mm2(1, 1)
+        mm1(0, 7)
+        mm1(1, 7)
+        quantise_t(7)
+        mm2(2, 1)
+        mm2(3, 1)
+        mm2(4, 1)
+        mm2(5, 1)
+        mm2(6, 0)
+        mm2(6, 1)
+        mm2(7, 0)
+        mm2(7, 1)
+
+        m8 = keep.tile([P, NB], F32, name="m8")
+        nc.vector.reduce_max(out=m8[:], in_=mx16[:].rearrange("p (b h) -> p b h", h=2), axis=AX.X)
+        rmax = keep.tile([P, 1], F32, name="rmax")
+        nc.vector.reduce_max(out=rmax[:], in_=mx16[:], axis=AX.X)
+        rb = keep.tile([P, P], F32, name="rb")
+        nc.vector.tensor_copy(out=rb[:], in_=rmax[:].to_broadcast([P, P]))
+        rbt = psum.tile([P, P], F32, name="rbt", tag="t")
+        nc.tensor.transpose(rbt[:], rb[:], ident[:])
+        gmax = keep.tile([P, 1], F32, name="gmax")
+        nc.vector.reduce_max(out=gmax[:], in_=rbt[:], axis=AX.X)
+        th = keep.tile([P, NB], F32, name="th")
+        nc.scalar.activation(out=th[:], in_=m8[:], func=ACT.Tanh)
+        ntg = keep.tile([P, 1], F32, name="ntg")
+        nc.scalar.activation(out=ntg[:], in_=gmax[:], func=ACT.Tanh, scale=-1.0)
+        rsum = keep.tile([P, 1], F32, name="rsum")
+        nc.scalar.activation(out=epad[:, 0:NB], in_=th[:], func=ACT.Exp, bias=ntg[:, 0:1], scale=1.0,
+                             accum_out=rsum[:])
+        tot = psum.tile([P, 1], F32, name="tot", tag="c")
+        nc.tensor.matmul(out=tot[:], lhsT=ones[:], rhs=rsum[:], start=True, stop=True)
+        et = psum.tile([P, P], F32, name="et", tag="t")
+        nc.tensor.transpose(et[:], epad[:], ident[:])
+        rc = keep.tile([P, 1], F32, name="rc")
+        nc.vector.reciprocal(out=rc[:], in_=tot[:])
+        res = keep.tile([P, P], F32, name="res")
+        nc.vector.tensor_scalar(out=res[:], in0=et[:], scalar1=rc[:, 0:1], scalar2=None, op0=ALU.mult)
+        nc.sync.dma_start(out=out_rows, in_=res[0:NB, :])

@@ -18,9 +18,40 @@ AX = mybir.AxisListType
 P = 128
 PACK = 4
 G = 2
-PIECE = 256
-NPIECE = 4
+QCOL = 256
+HCOL = 512
 NB = 8
+
+SCHEDULE = [
+    ("ld", "e", 0, 0), ("ld", "e", 0, 1), ("ld", "w", 0, 0), ("ld", "w", 0, 1),
+    ("ld", "w", 1, 0), ("ld", "w", 1, 1), ("ld", "e", 1, 0), ("ld", "e", 1, 1),
+    ("rg", "e", 0, 0, "v"), ("rg", "e", 1, 0, "s"), ("qz", "e", 0, 0), ("rg", "e", 0, 1, "v"),
+    ("rg", "e", 1, 1, "s"), ("qz", "e", 1, 0), ("qz", "e", 0, 1), ("rg", "w", 0, 0, "v"),
+    ("rg", "w", 1, 0, "s"), ("qz", "e", 1, 1), ("qz", "w", 0, 0), ("rg", "w", 0, 1, "v"),
+    ("rg", "w", 1, 1, "s"), ("qz", "w", 1, 0), ("qz", "w", 0, 1), ("qz", "w", 1, 1),
+    ("rg", "w", 3, 0, "s"), ("rg", "w", 2, 0, "v"), ("m1", 0, 0), ("qz", "w", 2, 0),
+    ("m1", 0, 1), ("rg", "w", 2, 1, "v"), ("rg", "w", 3, 1, "s"), ("m1", 0, 2),
+    ("qz", "w", 3, 0), ("m1", 0, 3), ("qz", "w", 2, 1), ("co", 0, 0),
+    ("qz", "w", 3, 1), ("rg", "e", 2, 0, "v"), ("co", 0, 1), ("m1", 1, 0),
+    ("qz", "e", 2, 0), ("co", 0, 2), ("m1", 1, 1), ("co", 0, 3),
+    ("rg", "e", 2, 1, "v"), ("m1", 1, 2), ("co", 1, 0), ("qz", "e", 2, 1),
+    ("m1", 1, 3), ("co", 1, 1), ("m1", 0, 5), ("co", 1, 2),
+    ("qt", 1), ("m1", 0, 4), ("rg", "e", 3, 0, "s"), ("qt", 2),
+    ("m2", 1, 0), ("qt", 0), ("m2", 2, 0), ("co", 1, 3),
+    ("rm", 1, 0), ("m1", 1, 4), ("rg", "e", 3, 1, "s"), ("qz", "e", 3, 0),
+    ("qt", 3), ("m1", 1, 5), ("m2", 0, 0), ("qz", "e", 3, 1),
+    ("co", 1, 5), ("rm", 2, 0), ("m2", 3, 0), ("co", 0, 5),
+    ("m2", 2, 1), ("rm", 0, 0), ("co", 0, 4), ("m2", 1, 1),
+    ("rm", 2, 1), ("co", 1, 4), ("m1", 0, 7), ("qt", 5),
+    ("rm", 1, 1), ("m1", 1, 6), ("rm", 3, 0), ("m1", 0, 6),
+    ("qt", 4), ("m2", 0, 1), ("co", 0, 6), ("m2", 3, 1),
+    ("rm", 0, 1), ("co", 1, 6), ("m2", 5, 0), ("co", 0, 7),
+    ("rm", 3, 1), ("m2", 4, 0), ("rm", 5, 0), ("m2", 4, 1),
+    ("rm", 4, 0), ("m1", 1, 7), ("qt", 6), ("m2", 5, 1),
+    ("rm", 4, 1), ("co", 1, 7), ("m2", 6, 0), ("rm", 5, 1),
+    ("m2", 6, 1), ("qt", 7), ("rm", 6, 0), ("m2", 7, 0),
+    ("rm", 6, 1), ("m2", 7, 1), ("rm", 7, 0), ("rm", 7, 1),
+]
 
 
 def tile_parallelcoattention_kernel(tc, embedding, heatm, W_b, out):
@@ -31,8 +62,8 @@ def tile_parallelcoattention_kernel(tc, embedding, heatm, W_b, out):
 
     with ExitStack() as ctx:
         keep = ctx.enter_context(tc.tile_pool(name="keep", bufs=1))
-        tpool = ctx.enter_context(tc.tile_pool(name="tpool", bufs=1))
         psum = ctx.enter_context(tc.psum_pool(name="psum", bufs=4))
+        ctx.enter_context(tc.manual_schedule())
 
         warm = keep.tile([P, 1], F32, name="warm")
         nc.vector.memset(warm[:], 0.0)
@@ -44,48 +75,54 @@ def tile_parallelcoattention_kernel(tc, embedding, heatm, W_b, out):
         nc.vector.memset(ones[:], 1.0)
         epad = keep.tile([P, P], F32, name="epad")
         nc.vector.memset(epad[:], 0.0)
+        mx16 = keep.tile([P, 2 * NB], F32, name="mx16")
 
         raw = {}
         grp = {}
         cod = {}
         scl = {}
-        order = [("e", 0), ("w", 0), ("w", 1), ("e", 1), ("w", 2), ("w", 3), ("e", 2), ("e", 3)]
-        for key in order:
-            kind, q = key
-            src = e_rows if kind == "e" else w_rows
-            raw[key] = keep.tile([P, G * PACK, PIECE], BF16, name="raw_%s%d" % key)
-            nc.sync.dma_start(out=raw[key][:], in_=src[:, :, q * PIECE:(q + 1) * PIECE])
-            grp[key] = keep.tile([P, G, PIECE, PACK], BF16, name="grp_%s%d" % key, align_bytes=64)
-            cod[key] = keep.tile([P, G, PIECE], U32, name="cod_%s%d" % key, align_bytes=64)
-            scl[key] = keep.tile([P, G, PIECE], U8, name="scl_%s%d" % key, align_bytes=64)
+        for kind in ("e", "w"):
+            for q in range(4):
+                key = (kind, q)
+                grp[key] = keep.tile([P, G, QCOL, PACK], BF16, name="grp_%s%d" % key, align_bytes=64)
+                cod[key] = keep.tile([P, G, QCOL], U32, name="cod_%s%d" % key, align_bytes=64)
+                scl[key] = keep.tile([P, G, QCOL], U8, name="scl_%s%d" % key, align_bytes=64)
+        tgr = {}
+        tcod = {}
+        tscl = {}
+        for b in range(NB):
+            tgr[b] = keep.tile([P, G, P, PACK], BF16, name="tgr%d" % b, align_bytes=64)
+            tcod[b] = keep.tile([P, G, P], U32, name="tcod%d" % b, align_bytes=64)
+            tscl[b] = keep.tile([P, G, P], U8, name="tscl%d" % b, align_bytes=64)
+        pts = {}
+        pcs = {}
 
-        def regroup(key, g, eng):
-            src = raw[key][:, g * PACK:(g + 1) * PACK, :].rearrange("p t (c i) -> p c t i", i=4)
-            dst = grp[key][:, g].rearrange("p (c i) t -> p c t i", i=4)
+        def load(kind, h, g):
+            rows = e_rows if kind == "e" else w_rows
+            raw[(kind, h, g)] = keep.tile([P, PACK, HCOL], BF16, name="raw_%s%d%d" % (kind, h, g))
+            nc.sync.dma_start(out=raw[(kind, h, g)][:],
+                              in_=rows[:, g * PACK:(g + 1) * PACK, h * HCOL:(h + 1) * HCOL])
+
+        def regroup(kind, q, g, eng):
+            cols = slice((q % 2) * QCOL, (q % 2) * QCOL + QCOL)
+            src = raw[(kind, q // 2, g)][:, :, cols].rearrange("p t (c i) -> p c t i", i=4)
+            dst = grp[(kind, q)][:, g].rearrange("p (c i) t -> p c t i", i=4)
             if eng == "v":
                 nc.vector.tensor_copy(out=dst, in_=src)
             else:
                 nc.scalar.copy(out=dst, in_=src)
 
-        def quantise(key, g):
+        def quantise(kind, q, g):
+            key = (kind, q)
             nc.vector.quantize_mx(
                 out=cod[key][:, g, :].bitcast(FP8X4),
                 scales=scl[key][:, g, :],
                 in_=grp[key][:, g].rearrange("p n t -> p (n t)"),
             )
 
-        def prepare(key):
-            regroup(key, 0, "v")
-            regroup(key, 1, "s")
-            quantise(key, 0)
-            quantise(key, 1)
-
-        tgr = {}
-        tcod = {}
-        tscl = {}
-
         def mm1(g2, b):
             pt = psum.tile([P, PACK, P], F32, name="pt", tag="t")
+            pts[(g2, b)] = pt
             ek = ("e", b // 2)
             ecol = slice((b % 2) * P, (b % 2) * P + P)
             for j in range(PACK):
@@ -101,23 +138,20 @@ def tile_parallelcoattention_kernel(tc, embedding, heatm, W_b, out):
                         start=(g1 == 0),
                         stop=(g1 == G - 1),
                     )
-            if b not in tgr:
-                tgr[b] = tpool.tile([P, G, P, PACK], BF16, name="tgr%d" % b, align_bytes=64)
-            nc.scalar.copy(out=tgr[b][:, g2], in_=pt[:].rearrange("p j n -> p n j"))
+
+        def copy_out(g2, b):
+            nc.scalar.copy(out=tgr[b][:, g2], in_=pts[(g2, b)][:].rearrange("p j n -> p n j"))
 
         def quantise_t(b):
-            tcod[b] = tpool.tile([P, G, P], U32, name="tcod%d" % b, align_bytes=64)
-            tscl[b] = tpool.tile([P, G, P], U8, name="tscl%d" % b, align_bytes=64)
             nc.vector.quantize_mx(
                 out=tcod[b][:].rearrange("p g n -> p (g n)").bitcast(FP8X4),
                 scales=tscl[b][:].rearrange("p g n -> p (g n)"),
                 in_=tgr[b][:].rearrange("p g n t -> p (g n t)"),
             )
 
-        mx16 = keep.tile([P, 2 * NB], F32, name="mx16")
-
         def mm2(b, h):
-            pc = psum.tile([P, 2, PIECE], F32, name="pc", tag="c")
+            pc = psum.tile([P, 2, QCOL], F32, name="pc", tag="c")
+            pcs[(b, h)] = pc
             for s in range(2):
                 ek = ("e", 2 * h + s)
                 for g2 in range(G):
@@ -130,51 +164,18 @@ def tile_parallelcoattention_kernel(tc, embedding, heatm, W_b, out):
                         start=(g2 == 0),
                         stop=(g2 == G - 1),
                     )
+
+        def row_max(b, h):
             nc.vector.reduce_max(
                 out=mx16[:, 2 * b + h:2 * b + h + 1],
-                in_=pc[:].rearrange("p s m -> p (s m)"),
+                in_=pcs[(b, h)][:].rearrange("p s m -> p (s m)"),
                 axis=AX.X,
             )
 
-        prepare(("e", 0))
-        prepare(("w", 0))
-        prepare(("w", 1))
-        mm1(0, 0)
-        mm1(0, 1)
-        prepare(("e", 1))
-        mm1(0, 2)
-        mm1(0, 3)
-        prepare(("w", 2))
-        prepare(("w", 3))
-        for b in range(4):
-            mm1(1, b)
-            quantise_t(b)
-        prepare(("e", 2))
-        for b in range(4):
-            mm2(b, 0)
-        for b in (4, 5):
-            mm1(0, b)
-            mm1(1, b)
-            quantise_t(b)
-        prepare(("e", 3))
-        mm2(4, 0)
-        mm2(5, 0)
-        mm1(0, 6)
-        mm1(1, 6)
-        quantise_t(6)
-        mm2(0, 1)
-        mm2(1, 1)
-        mm1(0, 7)
-        mm1(1, 7)
-        quantise_t(7)
-        mm2(2, 1)
-        mm2(3, 1)
-        mm2(4, 1)
-        mm2(5, 1)
-        mm2(6, 0)
-        mm2(6, 1)
-        mm2(7, 0)
-        mm2(7, 1)
+        steps = {"ld": load, "rg": regroup, "qz": quantise, "m1": mm1, "co": copy_out,
+                 "qt": quantise_t, "m2": mm2, "rm": row_max}
+        for step in SCHEDULE:
+            steps[step[0]](*step[1:])
 
         m8 = keep.tile([P, NB], F32, name="m8")
         nc.vector.reduce_max(out=m8[:], in_=mx16[:].rearrange("p (b h) -> p b h", h=2), axis=AX.X)

@@ -26,31 +26,31 @@ SCHEDULE = [
     ("ld", "e", 0, 0), ("ld", "e", 0, 1), ("ld", "w", 0, 0), ("ld", "w", 0, 1),
     ("ld", "w", 1, 0), ("ld", "w", 1, 1), ("ld", "e", 1, 0), ("ld", "e", 1, 1),
     ("rg", "e", 0, 0, "v"), ("rg", "e", 1, 0, "s"), ("qz", "e", 0, 0), ("rg", "e", 0, 1, "v"),
-    ("rg", "e", 1, 1, "s"), ("qz", "e", 1, 0), ("qz", "e", 0, 1), ("rg", "w", 0, 0, "v"),
-    ("rg", "w", 1, 0, "s"), ("qz", "e", 1, 1), ("qz", "w", 0, 0), ("rg", "w", 0, 1, "v"),
+    ("rg", "e", 1, 1, "s"), ("qz", "e", 1, 0), ("qz", "e", 0, 1), ("qz", "e", 1, 1),
+    ("rg", "w", 0, 0, "v"), ("rg", "w", 1, 0, "s"), ("qz", "w", 0, 0), ("rg", "w", 0, 1, "v"),
     ("rg", "w", 1, 1, "s"), ("qz", "w", 1, 0), ("qz", "w", 0, 1), ("qz", "w", 1, 1),
-    ("rg", "w", 3, 0, "s"), ("rg", "w", 2, 0, "v"), ("m1", 0, 0), ("qz", "w", 2, 0),
-    ("m1", 0, 1), ("rg", "w", 2, 1, "v"), ("rg", "w", 3, 1, "s"), ("m1", 0, 2),
-    ("qz", "w", 3, 0), ("m1", 0, 3), ("qz", "w", 2, 1), ("co", 0, 0),
-    ("qz", "w", 3, 1), ("rg", "e", 2, 0, "v"), ("co", 0, 1), ("m1", 1, 0),
-    ("qz", "e", 2, 0), ("co", 0, 2), ("m1", 1, 1), ("co", 0, 3),
-    ("rg", "e", 2, 1, "v"), ("m1", 1, 2), ("co", 1, 0), ("qz", "e", 2, 1),
-    ("m1", 1, 3), ("co", 1, 1), ("m1", 0, 5), ("co", 1, 2),
-    ("qt", 1), ("m1", 0, 4), ("rg", "e", 3, 0, "s"), ("qt", 2),
-    ("m2", 1, 0), ("qt", 0), ("m2", 2, 0), ("co", 1, 3),
-    ("rm", 1, 0), ("m1", 1, 4), ("rg", "e", 3, 1, "s"), ("qz", "e", 3, 0),
-    ("qt", 3), ("m1", 1, 5), ("m2", 0, 0), ("qz", "e", 3, 1),
-    ("co", 1, 5), ("rm", 2, 0), ("m2", 3, 0), ("co", 0, 5),
-    ("m2", 2, 1), ("rm", 0, 0), ("co", 0, 4), ("m2", 1, 1),
-    ("rm", 2, 1), ("co", 1, 4), ("m1", 0, 7), ("qt", 5),
-    ("rm", 1, 1), ("m1", 1, 6), ("rm", 3, 0), ("m1", 0, 6),
-    ("qt", 4), ("m2", 0, 1), ("co", 0, 6), ("m2", 3, 1),
-    ("rm", 0, 1), ("co", 1, 6), ("m2", 5, 0), ("co", 0, 7),
-    ("rm", 3, 1), ("m2", 4, 0), ("rm", 5, 0), ("m2", 4, 1),
-    ("rm", 4, 0), ("m1", 1, 7), ("qt", 6), ("m2", 5, 1),
-    ("rm", 4, 1), ("co", 1, 7), ("m2", 6, 0), ("rm", 5, 1),
-    ("m2", 6, 1), ("qt", 7), ("rm", 6, 0), ("m2", 7, 0),
-    ("rm", 6, 1), ("m2", 7, 1), ("rm", 7, 0), ("rm", 7, 1),
+    ("m1", 0, 0), ("m1", 0, 1), ("m1", 0, 2), ("m1", 0, 3),
+    ("rg", "w", 2, 0, "v"), ("rg", "w", 3, 0, "s"), ("qz", "w", 2, 0), ("rg", "w", 2, 1, "v"),
+    ("rg", "w", 3, 1, "s"), ("qz", "w", 3, 0), ("qz", "w", 2, 1), ("qz", "w", 3, 1),
+    ("co", 0, 0), ("co", 0, 1), ("co", 0, 2), ("co", 0, 3),
+    ("m1", 1, 0), ("m1", 1, 1), ("m1", 1, 2), ("m1", 1, 3),
+    ("rg", "e", 2, 0, "v"), ("qz", "e", 2, 0), ("rg", "e", 2, 1, "v"), ("qz", "e", 2, 1),
+    ("m1", 0, 4), ("m1", 0, 5), ("co", 1, 0), ("qt", 0),
+    ("co", 1, 1), ("qt", 1), ("co", 1, 2), ("qt", 2),
+    ("co", 1, 3), ("qt", 3), ("rg", "e", 3, 0, "s"), ("rg", "e", 3, 1, "s"),
+    ("m2", 0, 0), ("m2", 1, 0), ("m1", 1, 4), ("m2", 2, 0),
+    ("m1", 1, 5), ("m2", 3, 0), ("rm", 0, 0), ("rm", 1, 0),
+    ("qz", "e", 3, 0), ("qz", "e", 3, 1), ("rm", 2, 0), ("rm", 3, 0),
+    ("co", 0, 4), ("co", 1, 4), ("qt", 4), ("co", 0, 5),
+    ("co", 1, 5), ("qt", 5), ("m2", 0, 1), ("rm", 0, 1),
+    ("m2", 1, 1), ("rm", 1, 1), ("m2", 2, 1), ("rm", 2, 1),
+    ("m2", 3, 1), ("rm", 3, 1), ("m1", 0, 6), ("co", 0, 6),
+    ("m1", 1, 6), ("co", 1, 6), ("qt", 6), ("m2", 4, 0),
+    ("rm", 4, 0), ("m2", 4, 1), ("rm", 4, 1), ("m2", 5, 0),
+    ("rm", 5, 0), ("m2", 5, 1), ("rm", 5, 1), ("m1", 0, 7),
+    ("co", 0, 7), ("m1", 1, 7), ("co", 1, 7), ("qt", 7),
+    ("m2", 6, 0), ("rm", 6, 0), ("m2", 6, 1), ("rm", 6, 1),
+    ("m2", 7, 0), ("rm", 7, 0), ("m2", 7, 1), ("rm", 7, 1),
 ]
 
 
@@ -172,17 +172,23 @@ def tile_parallelcoattention_kernel(tc, embedding, heatm, W_b, out):
                 axis=AX.X,
             )
 
-        steps = {"ld": load, "rg": regroup, "qz": quantise, "m1": mm1, "co": copy_out,
+        def warm_up(kind, h, g, count):
+            junk = psum.tile([P, HCOL], F32, name="junk", tag="c")
+            for i in range(count):
+                nc.tensor.matmul(out=junk[:], lhsT=raw[(kind, h, g)][:, 0, 0:P], rhs=raw[(kind, h, g)][:, 1, :],
+                                 start=True, stop=True)
+
+        steps = {"wu": warm_up, "ld": load, "rg": regroup, "qz": quantise, "m1": mm1, "co": copy_out,
                  "qt": quantise_t, "m2": mm2, "rm": row_max}
         for step in SCHEDULE:
             steps[step[0]](*step[1:])
 
-        m8 = keep.tile([P, NB], F32, name="m8")
-        nc.vector.reduce_max(out=m8[:], in_=mx16[:].rearrange("p (b h) -> p b h", h=2), axis=AX.X)
         rmax = keep.tile([P, 1], F32, name="rmax")
         nc.vector.reduce_max(out=rmax[:], in_=mx16[:], axis=AX.X)
         rb = keep.tile([P, P], F32, name="rb")
         nc.vector.tensor_copy(out=rb[:], in_=rmax[:].to_broadcast([P, P]))
+        m8 = keep.tile([P, NB], F32, name="m8")
+        nc.vector.reduce_max(out=m8[:], in_=mx16[:].rearrange("p (b h) -> p b h", h=2), axis=AX.X)
         rbt = psum.tile([P, P], F32, name="rbt", tag="t")
         nc.tensor.transpose(rbt[:], rb[:], ident[:])
         gmax = keep.tile([P, 1], F32, name="gmax")
@@ -194,10 +200,10 @@ def tile_parallelcoattention_kernel(tc, embedding, heatm, W_b, out):
         rsum = keep.tile([P, 1], F32, name="rsum")
         nc.scalar.activation(out=epad[:, 0:NB], in_=th[:], func=ACT.Exp, bias=ntg[:, 0:1], scale=1.0,
                              accum_out=rsum[:])
-        tot = psum.tile([P, 1], F32, name="tot", tag="c")
-        nc.tensor.matmul(out=tot[:], lhsT=ones[:], rhs=rsum[:], start=True, stop=True)
         et = psum.tile([P, P], F32, name="et", tag="t")
         nc.tensor.transpose(et[:], epad[:], ident[:])
+        tot = psum.tile([P, 1], F32, name="tot", tag="c")
+        nc.tensor.matmul(out=tot[:], lhsT=ones[:], rhs=rsum[:], start=True, stop=True)
         rc = keep.tile([P, 1], F32, name="rc")
         nc.vector.reciprocal(out=rc[:], in_=tot[:])
         res = keep.tile([P, P], F32, name="res")

@@ -18,39 +18,52 @@ AX = mybir.AxisListType
 P = 128
 PACK = 4
 G = 2
-QCOL = 256
 HCOL = 512
 NB = 8
 
 SCHEDULE = [
     ("ld", "e", 0, 0), ("ld", "e", 0, 1), ("ld", "w", 0, 0), ("ld", "w", 0, 1),
     ("ld", "w", 1, 0), ("ld", "w", 1, 1), ("ld", "e", 1, 0), ("ld", "e", 1, 1),
-    ("rg", "e", 0, 0, "v"), ("rg", "e", 1, 0, "s"), ("qz", "e", 0, 0), ("rg", "e", 0, 1, "v"),
-    ("rg", "e", 1, 1, "s"), ("qz", "e", 1, 0), ("qz", "e", 0, 1), ("qz", "e", 1, 1),
-    ("rg", "w", 0, 0, "v"), ("rg", "w", 1, 0, "s"), ("qz", "w", 0, 0), ("rg", "w", 0, 1, "v"),
-    ("rg", "w", 1, 1, "s"), ("qz", "w", 1, 0), ("qz", "w", 0, 1), ("qz", "w", 1, 1),
-    ("m1", 0, 0), ("m1", 0, 1), ("m1", 0, 2), ("m1", 0, 3),
-    ("rg", "w", 2, 0, "v"), ("rg", "w", 3, 0, "s"), ("qz", "w", 2, 0), ("rg", "w", 2, 1, "v"),
-    ("rg", "w", 3, 1, "s"), ("qz", "w", 3, 0), ("qz", "w", 2, 1), ("qz", "w", 3, 1),
-    ("co", 0, 0), ("co", 0, 1), ("co", 0, 2), ("co", 0, 3),
-    ("m1", 1, 0), ("m1", 1, 1), ("m1", 1, 2), ("m1", 1, 3),
-    ("rg", "e", 2, 0, "v"), ("qz", "e", 2, 0), ("rg", "e", 2, 1, "v"), ("qz", "e", 2, 1),
-    ("m1", 0, 4), ("m1", 0, 5), ("co", 1, 0), ("qt", 0),
-    ("co", 1, 1), ("qt", 1), ("co", 1, 2), ("qt", 2),
-    ("co", 1, 3), ("qt", 3), ("rg", "e", 3, 0, "s"), ("rg", "e", 3, 1, "s"),
-    ("m2", 0, 0), ("m2", 1, 0), ("m1", 1, 4), ("m2", 2, 0),
-    ("m1", 1, 5), ("m2", 3, 0), ("rm", 0, 0), ("rm", 1, 0),
-    ("qz", "e", 3, 0), ("qz", "e", 3, 1), ("rm", 2, 0), ("rm", 3, 0),
-    ("co", 0, 4), ("co", 1, 4), ("qt", 4), ("co", 0, 5),
-    ("co", 1, 5), ("qt", 5), ("m2", 0, 1), ("rm", 0, 1),
-    ("m2", 1, 1), ("rm", 1, 1), ("m2", 2, 1), ("rm", 2, 1),
-    ("m2", 3, 1), ("rm", 3, 1), ("m1", 0, 6), ("co", 0, 6),
-    ("m1", 1, 6), ("co", 1, 6), ("qt", 6), ("m2", 4, 0),
-    ("rm", 4, 0), ("m2", 4, 1), ("rm", 4, 1), ("m2", 5, 0),
-    ("rm", 5, 0), ("m2", 5, 1), ("rm", 5, 1), ("m1", 0, 7),
-    ("co", 0, 7), ("m1", 1, 7), ("co", 1, 7), ("qt", 7),
-    ("m2", 6, 0), ("rm", 6, 0), ("m2", 6, 1), ("rm", 6, 1),
-    ("m2", 7, 0), ("rm", 7, 0), ("m2", 7, 1), ("rm", 7, 1),
+    ("rg", "e", 0, 0, 2, "v"), ("rg", "e", 0, 2, 2, "s"), ("qz", "e", 0, 0, 2), ("rg", "e", 1, 0, 2, "v"),
+    ("rg", "e", 1, 2, 2, "s"), ("qz", "e", 0, 2, 2), ("qz", "e", 1, 0, 2), ("rg", "w", 0, 0, 2, "v"),
+    ("rg", "w", 0, 2, 2, "s"), ("qz", "e", 1, 2, 2), ("qz", "w", 0, 0, 2), ("rg", "w", 1, 0, 1, "v"),
+    ("rg", "w", 1, 2, 1, "s"), ("rg", "w", 1, 1, 1, "v"), ("rg", "w", 1, 3, 1, "s"), ("qz", "w", 1, 0, 1),
+    ("qz", "w", 0, 2, 2), ("cell", 0, 0, 1), ("qz", "w", 1, 2, 1), ("cell", 0, 0, 3),
+    ("qz", "w", 1, 1, 1), ("rg", "w", 0, 6, 2, "s"), ("cell", 0, 0, 2), ("rg", "w", 0, 4, 2, "v"),
+    ("cell", 0, 2, 3), ("cell", 0, 1, 1), ("cell", 0, 1, 2), ("cell", 0, 2, 0),
+    ("qz", "w", 1, 3, 1), ("cell", 0, 2, 1), ("qz", "w", 0, 4, 2), ("cell", 0, 2, 2),
+    ("cell", 0, 3, 3), ("rg", "w", 1, 4, 1, "v"), ("rg", "w", 1, 6, 1, "s"), ("cell", 0, 3, 2),
+    ("cell", 0, 3, 1), ("rg", "w", 1, 5, 1, "v"), ("cell", 0, 0, 0), ("cell", 0, 3, 0),
+    ("rg", "w", 1, 7, 1, "s"), ("qz", "w", 1, 4, 1), ("cell", 0, 1, 0), ("qz", "w", 0, 6, 2),
+    ("cell", 0, 1, 3), ("cell", 1, 0, 0), ("qz", "w", 1, 5, 1), ("co", 0, 2),
+    ("cell", 1, 0, 2), ("rg", "e", 0, 4, 2, "v"), ("cell", 1, 1, 0), ("cell", 1, 0, 1),
+    ("co", 0, 1), ("cell", 1, 1, 2), ("qz", "w", 1, 6, 1), ("cell", 1, 0, 3),
+    ("qz", "w", 1, 7, 1), ("cell", 1, 1, 1), ("qz", "e", 0, 4, 2), ("cell", 1, 2, 0),
+    ("co", 0, 3), ("cell", 1, 3, 3), ("rg", "e", 1, 4, 2, "v"), ("cell", 1, 3, 1),
+    ("cell", 1, 2, 1), ("cell", 1, 2, 2), ("co", 0, 0), ("cell", 1, 3, 2),
+    ("qz", "e", 1, 4, 2), ("cell", 1, 3, 0), ("cell", 1, 2, 3), ("co", 1, 2),
+    ("rg", "e", 0, 6, 2, "v"), ("cell", 1, 1, 3), ("cell", 1, 2, 4), ("cell", 1, 3, 5),
+    ("cell", 0, 2, 5), ("co", 1, 0), ("rg", "e", 1, 6, 2, "v"), ("cell", 1, 0, 4),
+    ("cell", 0, 3, 5), ("cell", 1, 2, 5), ("co", 1, 1), ("cell", 0, 2, 4),
+    ("qt", 2), ("cell", 1, 1, 4), ("qz", "e", 0, 6, 2), ("cell", 1, 1, 5),
+    ("cell", 1, 0, 5), ("qz", "e", 1, 6, 2), ("cell", 0, 0, 5), ("cell", 1, 3, 4),
+    ("co", 1, 5), ("qt", 1), ("cell", 0, 1, 5), ("m2", 2, 0),
+    ("co", 1, 3), ("cell", 1, 0, 6), ("cell", 0, 1, 4), ("cell", 0, 0, 4),
+    ("co", 1, 4), ("qt", 3), ("cell", 0, 3, 4), ("m2", 1, 1),
+    ("qt", 0), ("co", 0, 5), ("rm", 2, 0), ("m2", 1, 0),
+    ("co", 0, 4), ("qt", 5), ("m2", 3, 0), ("rm", 1, 1),
+    ("cell", 1, 2, 6), ("cell", 1, 1, 6), ("rm", 3, 0), ("cell", 0, 1, 6),
+    ("cell", 1, 3, 6), ("cell", 0, 3, 6), ("m2", 5, 0), ("co", 1, 6),
+    ("rm", 1, 0), ("m2", 0, 0), ("qt", 4), ("cell", 1, 1, 7),
+    ("cell", 0, 0, 6), ("rm", 0, 0), ("cell", 0, 2, 6), ("m2", 3, 1),
+    ("co", 0, 6), ("rm", 5, 0), ("cell", 0, 1, 7), ("m2", 0, 1),
+    ("qt", 6), ("cell", 0, 3, 7), ("rm", 3, 1), ("m2", 4, 1),
+    ("rm", 0, 1), ("cell", 1, 0, 7), ("cell", 0, 2, 7), ("cell", 1, 3, 7),
+    ("m2", 4, 0), ("rm", 4, 1), ("cell", 1, 2, 7), ("m2", 2, 1),
+    ("rm", 4, 0), ("co", 1, 7), ("cell", 0, 0, 7), ("m2", 5, 1),
+    ("rm", 2, 1), ("co", 0, 7), ("m2", 6, 0), ("rm", 5, 1),
+    ("m2", 6, 1), ("qt", 7), ("rm", 6, 0), ("m2", 7, 1),
+    ("rm", 6, 1), ("m2", 7, 0), ("rm", 7, 1), ("rm", 7, 0),
 ]
 
 
@@ -62,7 +75,7 @@ def tile_parallelcoattention_kernel(tc, embedding, heatm, W_b, out):
 
     with ExitStack() as ctx:
         keep = ctx.enter_context(tc.tile_pool(name="keep", bufs=1))
-        psum = ctx.enter_context(tc.psum_pool(name="psum", bufs=4))
+        psum = ctx.enter_context(tc.psum_pool(name="psum", bufs=8))
         ctx.enter_context(tc.manual_schedule())
 
         warm = keep.tile([P, 1], F32, name="warm")
@@ -82,11 +95,11 @@ def tile_parallelcoattention_kernel(tc, embedding, heatm, W_b, out):
         cod = {}
         scl = {}
         for kind in ("e", "w"):
-            for q in range(4):
-                key = (kind, q)
-                grp[key] = keep.tile([P, G, QCOL, PACK], BF16, name="grp_%s%d" % key, align_bytes=64)
-                cod[key] = keep.tile([P, G, QCOL], U32, name="cod_%s%d" % key, align_bytes=64)
-                scl[key] = keep.tile([P, G, QCOL], U8, name="scl_%s%d" % key, align_bytes=64)
+            for h in range(2):
+                key = (kind, h)
+                grp[key] = keep.tile([P, G, HCOL, PACK], BF16, name="grp_%s%d" % key, align_bytes=64)
+                cod[key] = keep.tile([P, G, HCOL], U32, name="cod_%s%d" % key, align_bytes=64)
+                scl[key] = keep.tile([P, G, HCOL], U8, name="scl_%s%d" % key, align_bytes=64)
         tgr = {}
         tcod = {}
         tscl = {}
@@ -97,47 +110,44 @@ def tile_parallelcoattention_kernel(tc, embedding, heatm, W_b, out):
         pts = {}
         pcs = {}
 
+        def cols(c0, nchunk):
+            return slice((c0 % 4) * P, (c0 % 4 + nchunk) * P)
+
         def load(kind, h, g):
             rows = e_rows if kind == "e" else w_rows
             raw[(kind, h, g)] = keep.tile([P, PACK, HCOL], BF16, name="raw_%s%d%d" % (kind, h, g))
             nc.sync.dma_start(out=raw[(kind, h, g)][:],
                               in_=rows[:, g * PACK:(g + 1) * PACK, h * HCOL:(h + 1) * HCOL])
 
-        def regroup(kind, q, g, eng):
-            cols = slice((q % 2) * QCOL, (q % 2) * QCOL + QCOL)
-            src = raw[(kind, q // 2, g)][:, :, cols].rearrange("p t (c i) -> p c t i", i=4)
-            dst = grp[(kind, q)][:, g].rearrange("p (c i) t -> p c t i", i=4)
+        def regroup(kind, g, c0, nchunk, eng):
+            src = raw[(kind, c0 // 4, g)][:, :, cols(c0, nchunk)].rearrange("p t (c i) -> p c t i", i=4)
+            dst = grp[(kind, c0 // 4)][:, g, cols(c0, nchunk), :].rearrange("p (c i) t -> p c t i", i=4)
             if eng == "v":
                 nc.vector.tensor_copy(out=dst, in_=src)
             else:
                 nc.scalar.copy(out=dst, in_=src)
 
-        def quantise(kind, q, g):
-            key = (kind, q)
+        def quantise(kind, g, c0, nchunk):
+            key = (kind, c0 // 4)
             nc.vector.quantize_mx(
-                out=cod[key][:, g, :].bitcast(FP8X4),
-                scales=scl[key][:, g, :],
-                in_=grp[key][:, g].rearrange("p n t -> p (n t)"),
+                out=cod[key][:, g, cols(c0, nchunk)].bitcast(FP8X4),
+                scales=scl[key][:, g, cols(c0, nchunk)],
+                in_=grp[key][:, g, cols(c0, nchunk), :].rearrange("p n t -> p (n t)"),
             )
 
-        def mm1(g2, b):
-            pt = psum.tile([P, PACK, P], F32, name="pt", tag="t")
-            pts[(g2, b)] = pt
-            ek = ("e", b // 2)
-            ecol = slice((b % 2) * P, (b % 2) * P + P)
-            for j in range(PACK):
-                wk = ("w", 2 * g2 + j // 2)
-                wcol = slice((j % 2) * P, (j % 2) * P + P)
-                for g1 in range(G):
-                    nc.tensor.matmul_mx(
-                        out=pt[:, j, :],
-                        lhsT=cod[wk][:, g1, wcol].bitcast(FP8X4),
-                        lhsT_scale=scl[wk][:, g1, wcol],
-                        rhs=cod[ek][:, g1, ecol].bitcast(FP8X4),
-                        rhs_scale=scl[ek][:, g1, ecol],
-                        start=(g1 == 0),
-                        stop=(g1 == G - 1),
-                    )
+        def cell(g2, j, b):
+            if (g2, b) not in pts:
+                pts[(g2, b)] = psum.tile([P, PACK, P], F32, name="pt", tag="bank")
+            for g1 in range(G):
+                nc.tensor.matmul_mx(
+                    out=pts[(g2, b)][:, j, :],
+                    lhsT=cod[("w", g2)][:, g1, cols(j, 1)].bitcast(FP8X4),
+                    lhsT_scale=scl[("w", g2)][:, g1, cols(j, 1)],
+                    rhs=cod[("e", b // 4)][:, g1, cols(b, 1)].bitcast(FP8X4),
+                    rhs_scale=scl[("e", b // 4)][:, g1, cols(b, 1)],
+                    start=(g1 == 0),
+                    stop=(g1 == G - 1),
+                )
 
         def copy_out(g2, b):
             nc.scalar.copy(out=tgr[b][:, g2], in_=pts[(g2, b)][:].rearrange("p j n -> p n j"))
@@ -150,35 +160,29 @@ def tile_parallelcoattention_kernel(tc, embedding, heatm, W_b, out):
             )
 
         def mm2(b, h):
-            pc = psum.tile([P, 2, QCOL], F32, name="pc", tag="c")
+            pc = psum.tile([P, HCOL], F32, name="pc", tag="bank")
             pcs[(b, h)] = pc
-            for s in range(2):
-                ek = ("e", 2 * h + s)
-                for g2 in range(G):
-                    nc.tensor.matmul_mx(
-                        out=pc[:, s, :],
-                        lhsT=tcod[b][:, g2, :].bitcast(FP8X4),
-                        lhsT_scale=tscl[b][:, g2, :],
-                        rhs=cod[ek][:, g2, :].bitcast(FP8X4),
-                        rhs_scale=scl[ek][:, g2, :],
-                        start=(g2 == 0),
-                        stop=(g2 == G - 1),
-                    )
+            for g2 in range(G):
+                nc.tensor.matmul_mx(
+                    out=pc[:],
+                    lhsT=tcod[b][:, g2, :].bitcast(FP8X4),
+                    lhsT_scale=tscl[b][:, g2, :],
+                    rhs=cod[("e", h)][:, g2, :].bitcast(FP8X4),
+                    rhs_scale=scl[("e", h)][:, g2, :],
+                    start=(g2 == 0),
+                    stop=(g2 == G - 1),
+                )
 
         def row_max(b, h):
-            nc.vector.reduce_max(
-                out=mx16[:, 2 * b + h:2 * b + h + 1],
-                in_=pcs[(b, h)][:].rearrange("p s m -> p (s m)"),
-                axis=AX.X,
-            )
+            nc.vector.reduce_max(out=mx16[:, 2 * b + h:2 * b + h + 1], in_=pcs[(b, h)][:], axis=AX.X)
 
         def warm_up(kind, h, g, count):
-            junk = psum.tile([P, HCOL], F32, name="junk", tag="c")
+            junk = psum.tile([P, HCOL], F32, name="junk", tag="bank")
             for i in range(count):
                 nc.tensor.matmul(out=junk[:], lhsT=raw[(kind, h, g)][:, 0, 0:P], rhs=raw[(kind, h, g)][:, 1, :],
                                  start=True, stop=True)
 
-        steps = {"wu": warm_up, "ld": load, "rg": regroup, "qz": quantise, "m1": mm1, "co": copy_out,
+        steps = {"wu": warm_up, "ld": load, "rg": regroup, "qz": quantise, "cell": cell, "co": copy_out,
                  "qt": quantise_t, "m2": mm2, "rm": row_max}
         for step in SCHEDULE:
             steps[step[0]](*step[1:])
@@ -189,20 +193,20 @@ def tile_parallelcoattention_kernel(tc, embedding, heatm, W_b, out):
         nc.vector.tensor_copy(out=rb[:], in_=rmax[:].to_broadcast([P, P]))
         m8 = keep.tile([P, NB], F32, name="m8")
         nc.vector.reduce_max(out=m8[:], in_=mx16[:].rearrange("p (b h) -> p b h", h=2), axis=AX.X)
-        rbt = psum.tile([P, P], F32, name="rbt", tag="t")
+        rbt = psum.tile([P, P], F32, name="rbt", tag="bank")
         nc.tensor.transpose(rbt[:], rb[:], ident[:])
         gmax = keep.tile([P, 1], F32, name="gmax")
         nc.vector.reduce_max(out=gmax[:], in_=rbt[:], axis=AX.X)
         th = keep.tile([P, NB], F32, name="th")
         nc.scalar.activation(out=th[:], in_=m8[:], func=ACT.Tanh)
-        ntg = keep.tile([P, 1], F32, name="ntg")
-        nc.scalar.activation(out=ntg[:], in_=gmax[:], func=ACT.Tanh, scale=-1.0)
+        shift = keep.tile([P, 1], F32, name="shift")
+        nc.scalar.activation(out=shift[:], in_=gmax[:], func=ACT.Tanh, scale=-1.0)
         rsum = keep.tile([P, 1], F32, name="rsum")
-        nc.scalar.activation(out=epad[:, 0:NB], in_=th[:], func=ACT.Exp, bias=ntg[:, 0:1], scale=1.0,
+        nc.scalar.activation(out=epad[:, 0:NB], in_=th[:], func=ACT.Exp, bias=shift[:, 0:1], scale=1.0,
                              accum_out=rsum[:])
-        et = psum.tile([P, P], F32, name="et", tag="t")
+        et = psum.tile([P, P], F32, name="et", tag="bank")
         nc.tensor.transpose(et[:], epad[:], ident[:])
-        tot = psum.tile([P, 1], F32, name="tot", tag="c")
+        tot = psum.tile([P, 1], F32, name="tot", tag="bank")
         nc.tensor.matmul(out=tot[:], lhsT=ones[:], rhs=rsum[:], start=True, stop=True)
         rc = keep.tile([P, 1], F32, name="rc")
         nc.vector.reciprocal(out=rc[:], in_=tot[:])

@@ -88,6 +88,8 @@ def tile_parallelcoattention_kernel(tc, embedding, heatm, W_b, out):
         nc.vector.memset(ones[:], 1.0)
         epad = keep.tile([P, P], F32, name="epad")
         nc.vector.memset(epad[:], 0.0)
+        shift = keep.tile([P, 1], F32, name="shift")
+        nc.vector.memset(shift[:], -1.0)
         mx16 = keep.tile([P, 2 * NB], F32, name="mx16")
 
         raw = {}
@@ -187,20 +189,10 @@ def tile_parallelcoattention_kernel(tc, embedding, heatm, W_b, out):
         for step in SCHEDULE:
             steps[step[0]](*step[1:])
 
-        rmax = keep.tile([P, 1], F32, name="rmax")
-        nc.vector.reduce_max(out=rmax[:], in_=mx16[:], axis=AX.X)
-        rb = keep.tile([P, P], F32, name="rb")
-        nc.vector.tensor_copy(out=rb[:], in_=rmax[:].to_broadcast([P, P]))
         m8 = keep.tile([P, NB], F32, name="m8")
         nc.vector.reduce_max(out=m8[:], in_=mx16[:].rearrange("p (b h) -> p b h", h=2), axis=AX.X)
-        rbt = psum.tile([P, P], F32, name="rbt", tag="bank")
-        nc.tensor.transpose(rbt[:], rb[:], ident[:])
-        gmax = keep.tile([P, 1], F32, name="gmax")
-        nc.vector.reduce_max(out=gmax[:], in_=rbt[:], axis=AX.X)
         th = keep.tile([P, NB], F32, name="th")
         nc.scalar.activation(out=th[:], in_=m8[:], func=ACT.Tanh)
-        shift = keep.tile([P, 1], F32, name="shift")
-        nc.scalar.activation(out=shift[:], in_=gmax[:], func=ACT.Tanh, scale=-1.0)
         rsum = keep.tile([P, 1], F32, name="rsum")
         nc.scalar.activation(out=epad[:, 0:NB], in_=th[:], func=ACT.Exp, bias=shift[:, 0:1], scale=1.0,
                              accum_out=rsum[:])

@@ -24,46 +24,47 @@ NB = 8
 SCHEDULE = [
     ("ld", "e", 0, 0), ("ld", "e", 0, 1), ("ld", "w", 0, 0), ("ld", "w", 0, 1),
     ("ld", "w", 1, 0), ("ld", "w", 1, 1), ("ld", "e", 1, 0), ("ld", "e", 1, 1),
-    ("rg", "e", 0, 0, 2, "v"), ("rg", "e", 0, 2, 2, "s"), ("qz", "e", 0, 0, 2), ("rg", "e", 1, 0, 2, "v"),
-    ("rg", "e", 1, 2, 2, "s"), ("qz", "e", 0, 2, 2), ("qz", "e", 1, 0, 2), ("rg", "w", 0, 0, 2, "v"),
-    ("rg", "w", 0, 2, 2, "s"), ("qz", "e", 1, 2, 2), ("qz", "w", 0, 0, 2), ("rg", "w", 1, 0, 1, "v"),
-    ("rg", "w", 1, 2, 1, "s"), ("rg", "w", 1, 1, 1, "v"), ("rg", "w", 1, 3, 1, "s"), ("qz", "w", 1, 0, 1),
-    ("qz", "w", 0, 2, 2), ("cell", 0, 0, 1), ("qz", "w", 1, 2, 1), ("cell", 0, 0, 3),
-    ("qz", "w", 1, 1, 1), ("rg", "w", 0, 6, 2, "s"), ("cell", 0, 0, 2), ("rg", "w", 0, 4, 2, "v"),
-    ("cell", 0, 2, 3), ("cell", 0, 1, 1), ("cell", 0, 1, 2), ("cell", 0, 2, 0),
-    ("qz", "w", 1, 3, 1), ("cell", 0, 2, 1), ("qz", "w", 0, 4, 2), ("cell", 0, 2, 2),
-    ("cell", 0, 3, 3), ("rg", "w", 1, 4, 1, "v"), ("rg", "w", 1, 6, 1, "s"), ("cell", 0, 3, 2),
-    ("cell", 0, 3, 1), ("rg", "w", 1, 5, 1, "v"), ("cell", 0, 0, 0), ("cell", 0, 3, 0),
-    ("rg", "w", 1, 7, 1, "s"), ("qz", "w", 1, 4, 1), ("cell", 0, 1, 0), ("qz", "w", 0, 6, 2),
-    ("cell", 0, 1, 3), ("cell", 1, 0, 0), ("qz", "w", 1, 5, 1), ("co", 0, 2),
-    ("cell", 1, 0, 2), ("rg", "e", 0, 4, 2, "v"), ("cell", 1, 1, 0), ("cell", 1, 0, 1),
-    ("co", 0, 1), ("cell", 1, 1, 2), ("qz", "w", 1, 6, 1), ("cell", 1, 0, 3),
-    ("qz", "w", 1, 7, 1), ("cell", 1, 1, 1), ("qz", "e", 0, 4, 2), ("cell", 1, 2, 0),
-    ("co", 0, 3), ("cell", 1, 3, 3), ("rg", "e", 1, 4, 2, "v"), ("cell", 1, 3, 1),
-    ("cell", 1, 2, 1), ("cell", 1, 2, 2), ("co", 0, 0), ("cell", 1, 3, 2),
-    ("qz", "e", 1, 4, 2), ("cell", 1, 3, 0), ("cell", 1, 2, 3), ("co", 1, 2),
-    ("rg", "e", 0, 6, 2, "v"), ("cell", 1, 1, 3), ("cell", 1, 2, 4), ("cell", 1, 3, 5),
-    ("cell", 0, 2, 5), ("co", 1, 0), ("rg", "e", 1, 6, 2, "v"), ("cell", 1, 0, 4),
-    ("cell", 0, 3, 5), ("cell", 1, 2, 5), ("co", 1, 1), ("cell", 0, 2, 4),
-    ("qt", 2), ("cell", 1, 1, 4), ("qz", "e", 0, 6, 2), ("cell", 1, 1, 5),
-    ("cell", 1, 0, 5), ("qz", "e", 1, 6, 2), ("cell", 0, 0, 5), ("cell", 1, 3, 4),
-    ("co", 1, 5), ("qt", 1), ("cell", 0, 1, 5), ("m2", 2, 0),
-    ("co", 1, 3), ("cell", 1, 0, 6), ("cell", 0, 1, 4), ("cell", 0, 0, 4),
-    ("co", 1, 4), ("qt", 3), ("cell", 0, 3, 4), ("m2", 1, 1),
-    ("qt", 0), ("co", 0, 5), ("rm", 2, 0), ("m2", 1, 0),
-    ("co", 0, 4), ("qt", 5), ("m2", 3, 0), ("rm", 1, 1),
-    ("cell", 1, 2, 6), ("cell", 1, 1, 6), ("rm", 3, 0), ("cell", 0, 1, 6),
-    ("cell", 1, 3, 6), ("cell", 0, 3, 6), ("m2", 5, 0), ("co", 1, 6),
-    ("rm", 1, 0), ("m2", 0, 0), ("qt", 4), ("cell", 1, 1, 7),
-    ("cell", 0, 0, 6), ("rm", 0, 0), ("cell", 0, 2, 6), ("m2", 3, 1),
-    ("co", 0, 6), ("rm", 5, 0), ("cell", 0, 1, 7), ("m2", 0, 1),
-    ("qt", 6), ("cell", 0, 3, 7), ("rm", 3, 1), ("m2", 4, 1),
-    ("rm", 0, 1), ("cell", 1, 0, 7), ("cell", 0, 2, 7), ("cell", 1, 3, 7),
-    ("m2", 4, 0), ("rm", 4, 1), ("cell", 1, 2, 7), ("m2", 2, 1),
-    ("rm", 4, 0), ("co", 1, 7), ("cell", 0, 0, 7), ("m2", 5, 1),
-    ("rm", 2, 1), ("co", 0, 7), ("m2", 6, 0), ("rm", 5, 1),
-    ("m2", 6, 1), ("qt", 7), ("rm", 6, 0), ("m2", 7, 1),
-    ("rm", 6, 1), ("m2", 7, 0), ("rm", 7, 1), ("rm", 7, 0),
+    ("wu", "e", 0, 1, 4), ("wu", "w", 0, 0, 4), ("wu", "w", 0, 1, 2), ("rg", "e", 0, 0, 2, "v"),
+    ("rg", "e", 0, 2, 2, "s"), ("qz", "e", 0, 0, 2), ("rg", "e", 1, 0, 2, "v"), ("rg", "e", 1, 2, 2, "s"),
+    ("qz", "e", 0, 2, 2), ("qz", "e", 1, 0, 2), ("rg", "w", 0, 0, 2, "v"), ("rg", "w", 0, 2, 2, "s"),
+    ("qz", "e", 1, 2, 2), ("qz", "w", 0, 0, 2), ("rg", "w", 1, 0, 1, "v"), ("rg", "w", 1, 2, 1, "s"),
+    ("rg", "w", 1, 1, 1, "v"), ("rg", "w", 1, 3, 1, "s"), ("qz", "w", 1, 0, 1), ("qz", "w", 0, 2, 2),
+    ("cell", 0, 0, 1), ("qz", "w", 1, 2, 1), ("cell", 0, 0, 3), ("qz", "w", 1, 1, 1),
+    ("rg", "w", 0, 6, 2, "s"), ("cell", 0, 0, 2), ("rg", "w", 0, 4, 2, "v"), ("cell", 0, 2, 3),
+    ("cell", 0, 1, 1), ("cell", 0, 1, 2), ("cell", 0, 2, 0), ("qz", "w", 1, 3, 1),
+    ("cell", 0, 2, 1), ("qz", "w", 0, 4, 2), ("cell", 0, 2, 2), ("cell", 0, 3, 3),
+    ("rg", "w", 1, 4, 1, "v"), ("rg", "w", 1, 6, 1, "s"), ("cell", 0, 3, 2), ("cell", 0, 3, 1),
+    ("rg", "w", 1, 5, 1, "v"), ("cell", 0, 0, 0), ("cell", 0, 3, 0), ("rg", "w", 1, 7, 1, "s"),
+    ("qz", "w", 1, 4, 1), ("cell", 0, 1, 0), ("qz", "w", 0, 6, 2), ("cell", 0, 1, 3),
+    ("cell", 1, 0, 0), ("qz", "w", 1, 5, 1), ("co", 0, 2), ("cell", 1, 0, 2),
+    ("rg", "e", 0, 4, 2, "v"), ("cell", 1, 1, 0), ("cell", 1, 0, 1), ("co", 0, 1),
+    ("cell", 1, 1, 2), ("qz", "w", 1, 6, 1), ("cell", 1, 0, 3), ("qz", "w", 1, 7, 1),
+    ("cell", 1, 1, 1), ("qz", "e", 0, 4, 2), ("cell", 1, 2, 0), ("co", 0, 3),
+    ("cell", 1, 3, 3), ("rg", "e", 1, 4, 2, "v"), ("cell", 1, 3, 1), ("cell", 1, 2, 1),
+    ("cell", 1, 2, 2), ("co", 0, 0), ("cell", 1, 3, 2), ("qz", "e", 1, 4, 2),
+    ("cell", 1, 3, 0), ("cell", 1, 2, 3), ("co", 1, 2), ("rg", "e", 0, 6, 2, "v"),
+    ("cell", 1, 1, 3), ("cell", 1, 2, 4), ("cell", 1, 3, 5), ("cell", 0, 2, 5),
+    ("co", 1, 0), ("rg", "e", 1, 6, 2, "v"), ("cell", 1, 0, 4), ("cell", 0, 3, 5),
+    ("cell", 1, 2, 5), ("co", 1, 1), ("cell", 0, 2, 4), ("qt", 2),
+    ("cell", 1, 1, 4), ("qz", "e", 0, 6, 2), ("cell", 1, 1, 5), ("cell", 1, 0, 5),
+    ("qz", "e", 1, 6, 2), ("cell", 0, 0, 5), ("cell", 1, 3, 4), ("co", 1, 5),
+    ("qt", 1), ("cell", 0, 1, 5), ("m2", 2, 0), ("co", 1, 3),
+    ("cell", 1, 0, 6), ("cell", 0, 1, 4), ("cell", 0, 0, 4), ("co", 1, 4),
+    ("qt", 3), ("cell", 0, 3, 4), ("m2", 1, 1), ("qt", 0),
+    ("co", 0, 5), ("rm", 2, 0), ("m2", 1, 0), ("co", 0, 4),
+    ("qt", 5), ("m2", 3, 0), ("rm", 1, 1), ("cell", 1, 2, 6),
+    ("cell", 1, 1, 6), ("rm", 3, 0), ("cell", 0, 1, 6), ("cell", 1, 3, 6),
+    ("cell", 0, 3, 6), ("m2", 5, 0), ("co", 1, 6), ("rm", 1, 0),
+    ("m2", 0, 0), ("qt", 4), ("cell", 1, 1, 7), ("cell", 0, 0, 6),
+    ("rm", 0, 0), ("cell", 0, 2, 6), ("m2", 3, 1), ("co", 0, 6),
+    ("rm", 5, 0), ("cell", 0, 1, 7), ("m2", 0, 1), ("qt", 6),
+    ("cell", 0, 3, 7), ("rm", 3, 1), ("m2", 4, 1), ("rm", 0, 1),
+    ("cell", 1, 0, 7), ("cell", 0, 2, 7), ("cell", 1, 3, 7), ("m2", 4, 0),
+    ("rm", 4, 1), ("cell", 1, 2, 7), ("m2", 2, 1), ("rm", 4, 0),
+    ("co", 1, 7), ("cell", 0, 0, 7), ("m2", 5, 1), ("rm", 2, 1),
+    ("co", 0, 7), ("m2", 6, 0), ("rm", 5, 1), ("m2", 6, 1),
+    ("qt", 7), ("rm", 6, 0), ("m2", 7, 1), ("rm", 6, 1),
+    ("m2", 7, 0), ("rm", 7, 1), ("rm", 7, 0),
 ]
 
 

@@ -17,192 +17,231 @@ AX = mybir.AxisListType
 
 P = 128
 PACK = 4
-G = 2
-HCOL = 512
-NB = 8
-
-SCHEDULE = [
-    ("ld", "e", 0, 0), ("ld", "e", 0, 1), ("ld", "w", 0, 0), ("ld", "w", 0, 1),
-    ("ld", "w", 1, 0), ("ld", "w", 1, 1), ("ld", "e", 1, 0), ("ld", "e", 1, 1),
-    ("wu", "e", 0, 1, 4), ("wu", "w", 0, 0, 4), ("wu", "w", 0, 1, 2), ("rg", "e", 0, 0, 2, "v"),
-    ("rg", "e", 0, 2, 2, "s"), ("qz", "e", 0, 0, 2), ("rg", "e", 1, 0, 2, "v"), ("rg", "e", 1, 2, 2, "s"),
-    ("qz", "e", 0, 2, 2), ("qz", "e", 1, 0, 2), ("rg", "w", 0, 0, 2, "v"), ("rg", "w", 0, 2, 2, "s"),
-    ("qz", "e", 1, 2, 2), ("qz", "w", 0, 0, 2), ("rg", "w", 1, 0, 1, "v"), ("rg", "w", 1, 2, 1, "s"),
-    ("rg", "w", 1, 1, 1, "v"), ("rg", "w", 1, 3, 1, "s"), ("qz", "w", 1, 0, 1), ("qz", "w", 0, 2, 2),
-    ("cell", 0, 0, 1), ("qz", "w", 1, 2, 1), ("cell", 0, 0, 3), ("qz", "w", 1, 1, 1),
-    ("rg", "w", 0, 6, 2, "s"), ("cell", 0, 0, 2), ("rg", "w", 0, 4, 2, "v"), ("cell", 0, 2, 3),
-    ("cell", 0, 1, 1), ("cell", 0, 1, 2), ("cell", 0, 2, 0), ("qz", "w", 1, 3, 1),
-    ("cell", 0, 2, 1), ("qz", "w", 0, 4, 2), ("cell", 0, 2, 2), ("cell", 0, 3, 3),
-    ("rg", "w", 1, 4, 1, "v"), ("rg", "w", 1, 6, 1, "s"), ("cell", 0, 3, 2), ("cell", 0, 3, 1),
-    ("rg", "w", 1, 5, 1, "v"), ("cell", 0, 0, 0), ("cell", 0, 3, 0), ("rg", "w", 1, 7, 1, "s"),
-    ("qz", "w", 1, 4, 1), ("cell", 0, 1, 0), ("qz", "w", 0, 6, 2), ("cell", 0, 1, 3),
-    ("cell", 1, 0, 0), ("qz", "w", 1, 5, 1), ("co", 0, 2), ("cell", 1, 0, 2),
-    ("rg", "e", 0, 4, 2, "v"), ("cell", 1, 1, 0), ("cell", 1, 0, 1), ("co", 0, 1),
-    ("cell", 1, 1, 2), ("qz", "w", 1, 6, 1), ("cell", 1, 0, 3), ("qz", "w", 1, 7, 1),
-    ("cell", 1, 1, 1), ("qz", "e", 0, 4, 2), ("cell", 1, 2, 0), ("co", 0, 3),
-    ("cell", 1, 3, 3), ("rg", "e", 1, 4, 2, "v"), ("cell", 1, 3, 1), ("cell", 1, 2, 1),
-    ("cell", 1, 2, 2), ("co", 0, 0), ("cell", 1, 3, 2), ("qz", "e", 1, 4, 2),
-    ("cell", 1, 3, 0), ("cell", 1, 2, 3), ("co", 1, 2), ("rg", "e", 0, 6, 2, "v"),
-    ("cell", 1, 1, 3), ("cell", 1, 2, 4), ("cell", 1, 3, 5), ("cell", 0, 2, 5),
-    ("co", 1, 0), ("rg", "e", 1, 6, 2, "v"), ("cell", 1, 0, 4), ("cell", 0, 3, 5),
-    ("cell", 1, 2, 5), ("co", 1, 1), ("cell", 0, 2, 4), ("qt", 2),
-    ("cell", 1, 1, 4), ("qz", "e", 0, 6, 2), ("cell", 1, 1, 5), ("cell", 1, 0, 5),
-    ("qz", "e", 1, 6, 2), ("cell", 0, 0, 5), ("cell", 1, 3, 4), ("co", 1, 5),
-    ("qt", 1), ("cell", 0, 1, 5), ("m2", 2, 0), ("co", 1, 3),
-    ("cell", 1, 0, 6), ("cell", 0, 1, 4), ("cell", 0, 0, 4), ("co", 1, 4),
-    ("qt", 3), ("cell", 0, 3, 4), ("m2", 1, 1), ("qt", 0),
-    ("co", 0, 5), ("rm", 2, 0), ("m2", 1, 0), ("co", 0, 4),
-    ("qt", 5), ("m2", 3, 0), ("rm", 1, 1), ("cell", 1, 2, 6),
-    ("cell", 1, 1, 6), ("rm", 3, 0), ("cell", 0, 1, 6), ("cell", 1, 3, 6),
-    ("cell", 0, 3, 6), ("m2", 5, 0), ("co", 1, 6), ("rm", 1, 0),
-    ("m2", 0, 0), ("qt", 4), ("cell", 1, 1, 7), ("cell", 0, 0, 6),
-    ("rm", 0, 0), ("cell", 0, 2, 6), ("m2", 3, 1), ("co", 0, 6),
-    ("rm", 5, 0), ("cell", 0, 1, 7), ("m2", 0, 1), ("qt", 6),
-    ("cell", 0, 3, 7), ("rm", 3, 1), ("m2", 4, 1), ("rm", 0, 1),
-    ("cell", 1, 0, 7), ("cell", 0, 2, 7), ("cell", 1, 3, 7), ("m2", 4, 0),
-    ("rm", 4, 1), ("cell", 1, 2, 7), ("m2", 2, 1), ("rm", 4, 0),
-    ("co", 1, 7), ("cell", 0, 0, 7), ("m2", 5, 1), ("rm", 2, 1),
-    ("co", 0, 7), ("m2", 6, 0), ("rm", 5, 1), ("m2", 6, 1),
-    ("qt", 7), ("rm", 6, 0), ("m2", 7, 1), ("rm", 6, 1),
-    ("m2", 7, 0), ("rm", 7, 1), ("rm", 7, 0),
-]
+PASSES = 2
+HALF = 512
+CHUNKS = 4
+BLOCKS = 8
+WEAVE = 2
+LAG = 2
 
 
 def tile_parallelcoattention_kernel(tc, embedding, heatm, W_b, out):
     nc = tc.nc
-    e_rows = embedding[0].rearrange("(r p) n -> p r n", p=P)
-    w_rows = W_b.rearrange("(r p) n -> p r n", p=P)
-    out_rows = out[0].rearrange("(c q) u -> c (q u)", c=NB)
+    dram_rows = {
+        "e": embedding[0].rearrange("(r p) n -> p r n", p=P),
+        "w": W_b.rearrange("(r p) n -> p r n", p=P),
+    }
+    out_rows = out[0].rearrange("(b q) u -> b (q u)", b=BLOCKS)
 
     with ExitStack() as ctx:
         keep = ctx.enter_context(tc.tile_pool(name="keep", bufs=1))
         psum = ctx.enter_context(tc.psum_pool(name="psum", bufs=8))
         ctx.enter_context(tc.manual_schedule())
 
-        warm = keep.tile([P, 1], F32, name="warm")
-        nc.vector.memset(warm[:], 0.0)
-        warm2 = keep.tile([P, 1], F32, name="warm2")
-        nc.scalar.activation(out=warm2[:], in_=warm[:], func=ACT.Tanh)
+        zero = keep.tile([P, 1], F32, name="zero")
+        nc.vector.memset(zero[:], 0.0)
+        table_load = keep.tile([P, 1], F32, name="table_load")
+        nc.scalar.activation(out=table_load[:], in_=zero[:], func=ACT.Tanh)
         ident = keep.tile([P, P], F32, name="ident")
         make_identity(nc, ident[:])
         ones = keep.tile([P, P], F32, name="ones")
         nc.vector.memset(ones[:], 1.0)
-        epad = keep.tile([P, P], F32, name="epad")
-        nc.vector.memset(epad[:], 0.0)
-        shift = keep.tile([P, 1], F32, name="shift")
-        nc.vector.memset(shift[:], -1.0)
-        mx16 = keep.tile([P, 2 * NB], F32, name="mx16")
+        expo = keep.tile([P, P], F32, name="expo")
+        nc.vector.memset(expo[:], 0.0)
+        minus_one = keep.tile([P, 1], F32, name="minus_one")
+        nc.vector.memset(minus_one[:], -1.0)
+        half_max = keep.tile([P, 2 * BLOCKS], F32, name="half_max")
 
         raw = {}
-        grp = {}
-        cod = {}
-        scl = {}
+        grouped = {}
+        codes = {}
+        scales = {}
         for kind in ("e", "w"):
-            for h in range(2):
-                key = (kind, h)
-                grp[key] = keep.tile([P, G, HCOL, PACK], BF16, name="grp_%s%d" % key, align_bytes=64)
-                cod[key] = keep.tile([P, G, HCOL], U32, name="cod_%s%d" % key, align_bytes=64)
-                scl[key] = keep.tile([P, G, HCOL], U8, name="scl_%s%d" % key, align_bytes=64)
-        tgr = {}
-        tcod = {}
-        tscl = {}
-        for b in range(NB):
-            tgr[b] = keep.tile([P, G, P, PACK], BF16, name="tgr%d" % b, align_bytes=64)
-            tcod[b] = keep.tile([P, G, P], U32, name="tcod%d" % b, align_bytes=64)
-            tscl[b] = keep.tile([P, G, P], U8, name="tscl%d" % b, align_bytes=64)
-        pts = {}
-        pcs = {}
+            for half in range(2):
+                key = (kind, half)
+                grouped[key] = keep.tile([P, PASSES, HALF, PACK], BF16, name="grouped_%s%d" % key, align_bytes=64)
+                codes[key] = keep.tile([P, PASSES, HALF], U32, name="codes_%s%d" % key, align_bytes=64)
+                scales[key] = keep.tile([P, PASSES, HALF], U8, name="scales_%s%d" % key, align_bytes=64)
+        t_grouped = {}
+        t_codes = {}
+        t_scales = {}
+        for b in range(BLOCKS):
+            t_grouped[b] = keep.tile([P, PASSES, P, PACK], BF16, name="t_grouped%d" % b, align_bytes=64)
+            t_codes[b] = keep.tile([P, PASSES, P], U32, name="t_codes%d" % b, align_bytes=64)
+            t_scales[b] = keep.tile([P, PASSES, P], U8, name="t_scales%d" % b, align_bytes=64)
+        t_banks = {}
+        c_banks = {}
+        early = list(range(CHUNKS))
+        late = list(range(CHUNKS, BLOCKS))
 
-        def cols(c0, nchunk):
-            return slice((c0 % 4) * P, (c0 % 4 + nchunk) * P)
+        def columns(chunk, count):
+            return slice((chunk % CHUNKS) * P, (chunk % CHUNKS + count) * P)
 
-        def load(kind, h, g):
-            rows = e_rows if kind == "e" else w_rows
-            raw[(kind, h, g)] = keep.tile([P, PACK, HCOL], BF16, name="raw_%s%d%d" % (kind, h, g))
-            nc.sync.dma_start(out=raw[(kind, h, g)][:],
-                              in_=rows[:, g * PACK:(g + 1) * PACK, h * HCOL:(h + 1) * HCOL])
+        def load(kind, half, g):
+            raw[(kind, half, g)] = keep.tile([P, PACK, HALF], BF16, name="raw_%s%d%d" % (kind, half, g))
+            nc.sync.dma_start(
+                out=raw[(kind, half, g)][:],
+                in_=dram_rows[kind][:, g * PACK:(g + 1) * PACK, half * HALF:(half + 1) * HALF],
+            )
 
-        def regroup(kind, g, c0, nchunk, eng):
-            src = raw[(kind, c0 // 4, g)][:, :, cols(c0, nchunk)].rearrange("p t (c i) -> p c t i", i=4)
-            dst = grp[(kind, c0 // 4)][:, g, cols(c0, nchunk), :].rearrange("p (c i) t -> p c t i", i=4)
-            if eng == "v":
+        def regroup(engine, kind, g, chunk, count):
+            half = chunk // CHUNKS
+            src = raw[(kind, half, g)][:, :, columns(chunk, count)].rearrange("p j (c i) -> p c j i", i=4)
+            dst = grouped[(kind, half)][:, g, columns(chunk, count), :].rearrange("p (c i) j -> p c j i", i=4)
+            if engine == "vector":
                 nc.vector.tensor_copy(out=dst, in_=src)
             else:
                 nc.scalar.copy(out=dst, in_=src)
 
-        def quantise(kind, g, c0, nchunk):
-            key = (kind, c0 // 4)
+        def quantise(kind, g, chunk, count):
+            key = (kind, chunk // CHUNKS)
             nc.vector.quantize_mx(
-                out=cod[key][:, g, cols(c0, nchunk)].bitcast(FP8X4),
-                scales=scl[key][:, g, cols(c0, nchunk)],
-                in_=grp[key][:, g, cols(c0, nchunk), :].rearrange("p n t -> p (n t)"),
+                out=codes[key][:, g, columns(chunk, count)].bitcast(FP8X4),
+                scales=scales[key][:, g, columns(chunk, count)],
+                in_=grouped[key][:, g, columns(chunk, count), :].rearrange("p n j -> p (n j)"),
             )
 
-        def cell(g2, j, b):
-            if (g2, b) not in pts:
-                pts[(g2, b)] = psum.tile([P, PACK, P], F32, name="pt", tag="bank")
-            for g1 in range(G):
+        def t_cell(g2, j, b):
+            if (g2, b) not in t_banks:
+                t_banks[(g2, b)] = psum.tile([P, PACK, P], F32, name="t_bank", tag="bank")
+            for g in range(PASSES):
                 nc.tensor.matmul_mx(
-                    out=pts[(g2, b)][:, j, :],
-                    lhsT=cod[("w", g2)][:, g1, cols(j, 1)].bitcast(FP8X4),
-                    lhsT_scale=scl[("w", g2)][:, g1, cols(j, 1)],
-                    rhs=cod[("e", b // 4)][:, g1, cols(b, 1)].bitcast(FP8X4),
-                    rhs_scale=scl[("e", b // 4)][:, g1, cols(b, 1)],
-                    start=(g1 == 0),
-                    stop=(g1 == G - 1),
+                    out=t_banks[(g2, b)][:, j, :],
+                    lhsT=codes[("w", g2)][:, g, columns(j, 1)].bitcast(FP8X4),
+                    lhsT_scale=scales[("w", g2)][:, g, columns(j, 1)],
+                    rhs=codes[("e", b // CHUNKS)][:, g, columns(b, 1)].bitcast(FP8X4),
+                    rhs_scale=scales[("e", b // CHUNKS)][:, g, columns(b, 1)],
+                    start=(g == 0),
+                    stop=(g == PASSES - 1),
                 )
 
-        def copy_out(g2, b):
-            nc.scalar.copy(out=tgr[b][:, g2], in_=pts[(g2, b)][:].rearrange("p j n -> p n j"))
+        def t_cells(g2, chunks, blocks):
+            for j in chunks:
+                for b in blocks:
+                    t_cell(g2, j, b)
+
+        def copy_out_t(g2, b):
+            nc.scalar.copy(out=t_grouped[b][:, g2], in_=t_banks[(g2, b)][:].rearrange("p j n -> p n j"))
 
         def quantise_t(b):
             nc.vector.quantize_mx(
-                out=tcod[b][:].rearrange("p g n -> p (g n)").bitcast(FP8X4),
-                scales=tscl[b][:].rearrange("p g n -> p (g n)"),
-                in_=tgr[b][:].rearrange("p g n t -> p (g n t)"),
+                out=t_codes[b][:].rearrange("p g n -> p (g n)").bitcast(FP8X4),
+                scales=t_scales[b][:].rearrange("p g n -> p (g n)"),
+                in_=t_grouped[b][:].rearrange("p g n j -> p (g n j)"),
             )
 
-        def mm2(b, h):
-            pc = psum.tile([P, HCOL], F32, name="pc", tag="bank")
-            pcs[(b, h)] = pc
-            for g2 in range(G):
+        def c_bank(b, half):
+            c_banks[(b, half)] = psum.tile([P, HALF], F32, name="c_bank", tag="bank")
+            for g2 in range(PASSES):
                 nc.tensor.matmul_mx(
-                    out=pc[:],
-                    lhsT=tcod[b][:, g2, :].bitcast(FP8X4),
-                    lhsT_scale=tscl[b][:, g2, :],
-                    rhs=cod[("e", h)][:, g2, :].bitcast(FP8X4),
-                    rhs_scale=scl[("e", h)][:, g2, :],
+                    out=c_banks[(b, half)][:],
+                    lhsT=t_codes[b][:, g2, :].bitcast(FP8X4),
+                    lhsT_scale=t_scales[b][:, g2, :],
+                    rhs=codes[("e", half)][:, g2, :].bitcast(FP8X4),
+                    rhs_scale=scales[("e", half)][:, g2, :],
                     start=(g2 == 0),
-                    stop=(g2 == G - 1),
+                    stop=(g2 == PASSES - 1),
                 )
 
-        def row_max(b, h):
-            nc.vector.reduce_max(out=mx16[:, 2 * b + h:2 * b + h + 1], in_=pcs[(b, h)][:], axis=AX.X)
+        def row_max(b, half):
+            nc.vector.reduce_max(out=half_max[:, 2 * b + half:2 * b + half + 1], in_=c_banks[(b, half)][:], axis=AX.X)
 
-        def warm_up(kind, h, g, count):
-            junk = psum.tile([P, HCOL], F32, name="junk", tag="bank")
+        def keep_clock_up(kind, half, g, count):
+            unread = psum.tile([P, HALF], F32, name="unread", tag="bank")
             for i in range(count):
-                nc.tensor.matmul(out=junk[:], lhsT=raw[(kind, h, g)][:, 0, 0:P], rhs=raw[(kind, h, g)][:, 1, :],
+                nc.tensor.matmul(out=unread[:], lhsT=raw[(kind, half, g)][:, 0, 0:P], rhs=raw[(kind, half, g)][:, 1, :],
                                  start=True, stop=True)
 
-        steps = {"wu": warm_up, "ld": load, "rg": regroup, "qz": quantise, "cell": cell, "co": copy_out,
-                 "qt": quantise_t, "m2": mm2, "rm": row_max}
-        for step in SCHEDULE:
-            steps[step[0]](*step[1:])
+        for kind, half in (("e", 0), ("w", 0), ("w", 1), ("e", 1)):
+            for g in range(PASSES):
+                load(kind, half, g)
+        keep_clock_up("e", 0, 1, 4)
+        keep_clock_up("w", 0, 0, 4)
+        keep_clock_up("w", 0, 1, 2)
 
-        m8 = keep.tile([P, NB], F32, name="m8")
-        nc.vector.reduce_max(out=m8[:], in_=mx16[:].rearrange("p (b h) -> p b h", h=2), axis=AX.X)
-        th = keep.tile([P, NB], F32, name="th")
-        nc.scalar.activation(out=th[:], in_=m8[:], func=ACT.Tanh)
-        rsum = keep.tile([P, 1], F32, name="rsum")
-        nc.scalar.activation(out=epad[:, 0:NB], in_=th[:], func=ACT.Exp, bias=shift[:, 0:1], scale=1.0,
-                             accum_out=rsum[:])
-        et = psum.tile([P, P], F32, name="et", tag="bank")
-        nc.tensor.transpose(et[:], epad[:], ident[:])
-        tot = psum.tile([P, 1], F32, name="tot", tag="bank")
-        nc.tensor.matmul(out=tot[:], lhsT=ones[:], rhs=rsum[:], start=True, stop=True)
-        rc = keep.tile([P, 1], F32, name="rc")
-        nc.vector.reciprocal(out=rc[:], in_=tot[:])
-        res = keep.tile([P, P], F32, name="res")
-        nc.vector.tensor_scalar(out=res[:], in0=et[:], scalar1=rc[:, 0:1], scalar2=None, op0=ALU.mult)
-        nc.sync.dma_start(out=out_rows, in_=res[0:NB, :])
+        regroup("vector", "e", 0, 0, 2)
+        regroup("scalar", "e", 0, 2, 2)
+        quantise("e", 0, 0, 2)
+        regroup("vector", "e", 1, 0, 2)
+        regroup("scalar", "e", 1, 2, 2)
+        quantise("e", 0, 2, 2)
+        quantise("e", 1, 0, 2)
+        left_over = [("e", 1, 2, 2)]
+        for half in range(2):
+            first = half * CHUNKS
+            regroup("vector", "w", 0, first, 2)
+            regroup("scalar", "w", 0, first + 2, 2)
+            for item in left_over:
+                quantise(*item)
+            quantise("w", 0, first, 2)
+            if half > 0:
+                t_cells(half - 1, (2, 3), early)
+            regroup("vector", "w", 1, first, 1)
+            regroup("vector", "w", 1, first + 1, 1)
+            regroup("scalar", "w", 1, first + 2, 1)
+            regroup("scalar", "w", 1, first + 3, 1)
+            quantise("w", 1, first, 1)
+            quantise("w", 0, first + 2, 2)
+            quantise("w", 1, first + 1, 1)
+            t_cells(half, (0, 1), early)
+            left_over = [("w", 1, first + 2, 1), ("w", 1, first + 3, 1)]
+        regroup("vector", "e", 0, 4, 2)
+        for item in left_over:
+            quantise(*item)
+        quantise("e", 0, 4, 2)
+        t_cells(1, (2, 3), early)
+        for b in early:
+            copy_out_t(0, b)
+        regroup("vector", "e", 1, 4, 2)
+        quantise("e", 1, 4, 2)
+        regroup("vector", "e", 0, 6, 2)
+        regroup("vector", "e", 1, 6, 2)
+        copy_out_t(1, 0)
+        quantise_t(0)
+        quantise("e", 0, 6, 2)
+        quantise("e", 1, 6, 2)
+        for b in early[1:]:
+            copy_out_t(1, b)
+            quantise_t(b)
+
+        late_cells = [(g2, j, b) for b in late for g2 in range(PASSES) for j in range(PACK)]
+        written = []
+        copied = []
+        quantised = []
+
+        def next_cells(count, bank_number):
+            for g2, j, b in late_cells[len(written):len(written) + count]:
+                t_cell(g2, j, b)
+                written.append((g2, j, b))
+                if j == PACK - 1:
+                    copy_out_t(g2, b)
+                    if g2 == PASSES - 1:
+                        copied.append((b, bank_number))
+
+        next_cells(3 * PACK, -1)
+        bank_order = [(b, half) for half in range(2) for b in early] + [(b, half) for b in late for half in range(2)]
+        for bank_number, (b, half) in enumerate(bank_order):
+            c_bank(b, half)
+            next_cells(WEAVE, bank_number)
+            for block, since in copied[len(quantised):]:
+                if bank_number - since >= LAG:
+                    quantise_t(block)
+                    quantised.append(block)
+            row_max(b, half)
+
+        block_max = keep.tile([P, BLOCKS], F32, name="block_max")
+        nc.vector.reduce_max(out=block_max[:], in_=half_max[:].rearrange("q (b h) -> q b h", h=2), axis=AX.X)
+        tanh_max = keep.tile([P, BLOCKS], F32, name="tanh_max")
+        nc.scalar.activation(out=tanh_max[:], in_=block_max[:], func=ACT.Tanh)
+        row_sum = keep.tile([P, 1], F32, name="row_sum")
+        nc.scalar.activation(out=expo[:, 0:BLOCKS], in_=tanh_max[:], func=ACT.Exp, bias=minus_one[:, 0:1], scale=1.0,
+                             accum_out=row_sum[:])
+        expo_t = psum.tile([P, P], F32, name="expo_t", tag="bank")
+        nc.tensor.transpose(expo_t[:], expo[:], ident[:])
+        total = psum.tile([P, 1], F32, name="total", tag="bank")
+        nc.tensor.matmul(out=total[:], lhsT=ones[:], rhs=row_sum[:], start=True, stop=True)
+        inverse = keep.tile([P, 1], F32, name="inverse")
+        nc.vector.reciprocal(out=inverse[:], in_=total[:])
+        result = keep.tile([P, P], F32, name="result")
+        nc.vector.tensor_scalar(out=result[:], in0=expo_t[:], scalar1=inverse[:, 0:1], scalar2=None, op0=ALU.mult)
+        nc.sync.dma_start(out=out_rows, in_=result[0:BLOCKS, :])

@@ -48,8 +48,6 @@ def tile_parallelcoattention_kernel(tc, embedding, heatm, W_b, out):
         nc.vector.memset(ones[:], 1.0)
         expo = keep.tile([P, P], F32, name="expo")
         nc.vector.memset(expo[:], 0.0)
-        minus_one = keep.tile([P, 1], F32, name="minus_one")
-        nc.vector.memset(minus_one[:], -1.0)
         half_max = keep.tile([P, 2 * BLOCKS], F32, name="half_max")
 
         raw = {}
@@ -229,12 +227,20 @@ def tile_parallelcoattention_kernel(tc, embedding, heatm, W_b, out):
                     quantised.append(block)
             row_max(b, half)
 
+        own_max = keep.tile([P, 1], F32, name="own_max")
+        nc.vector.reduce_max(out=own_max[:], in_=half_max[:], axis=AX.X)
+        all_max = psum.tile([P, P], F32, name="all_max", tag="bank")
+        nc.tensor.transpose(all_max[:], own_max[:, 0:1].to_broadcast([P, P]), ident[:])
         block_max = keep.tile([P, BLOCKS], F32, name="block_max")
         nc.vector.reduce_max(out=block_max[:], in_=half_max[:].rearrange("q (b h) -> q b h", h=2), axis=AX.X)
         tanh_max = keep.tile([P, BLOCKS], F32, name="tanh_max")
         nc.scalar.activation(out=tanh_max[:], in_=block_max[:], func=ACT.Tanh)
+        top = keep.tile([P, 1], F32, name="top")
+        nc.vector.reduce_max(out=top[:], in_=all_max[:], axis=AX.X)
+        minus_top = keep.tile([P, 1], F32, name="minus_top")
+        nc.scalar.activation(out=minus_top[:], in_=top[:], func=ACT.Tanh, scale=-1.0)
         row_sum = keep.tile([P, 1], F32, name="row_sum")
-        nc.scalar.activation(out=expo[:, 0:BLOCKS], in_=tanh_max[:], func=ACT.Exp, bias=minus_one[:, 0:1], scale=1.0,
+        nc.scalar.activation(out=expo[:, 0:BLOCKS], in_=tanh_max[:], func=ACT.Exp, bias=minus_top[:, 0:1], scale=1.0,
                              accum_out=row_sum[:])
         expo_t = psum.tile([P, P], F32, name="expo_t", tag="bank")
         nc.tensor.transpose(expo_t[:], expo[:], ident[:])

from contextlib import ExitStack

import concourse.mybir as mybir
from concourse.masks import make_identity

FLOPS = 2 * 2 * 1024 * 1024 * 1024
BYTES = 2 * 1024 * 1024 * 2 + 1024 * 4

F32 = mybir.dt.float32
BF16 = mybir.dt.bfloat16
U32 = mybir.dt.uint32
U8 = mybir.dt.uint8
FP8X4 = mybir.dt.float8_e4m3fn_x4
ACT = mybir.ActivationFunctionType
ALU = mybir.AluOpType
AX = mybir.AxisListType

P = 128
PACK = 4
PASSES = 2
HALF = 512
CHUNKS = 4
BLOCKS = 8
WEAVE = 2
LAG = 2


def tile_parallelcoattention_kernel(tc, embedding, heatm, W_b, out):
    nc = tc.nc
    dram_rows = {
        "e": embedding[0].rearrange("(r p) n -> p r n", p=P),
        "w": W_b.rearrange("(r p) n -> p r n", p=P),
    }
    out_rows = out[0].rearrange("(b q) u -> b (q u)", b=BLOCKS)

    with ExitStack() as ctx:
        keep = ctx.enter_context(tc.tile_pool(name="keep", bufs=1))
        psum = ctx.enter_context(tc.psum_pool(name="psum", bufs=8))
        ctx.enter_context(tc.manual_schedule())

        zero = keep.tile([P, 1], F32, name="zero")
        nc.vector.memset(zero[:], 0.0)
        table_load = keep.tile([P, 1], F32, name="table_load")
        nc.scalar.activation(out=table_load[:], in_=zero[:], func=ACT.Tanh)
        ident = keep.tile([P, P], F32, name="ident")
        make_identity(nc, ident[:])
        ones = keep.tile([P, P], F32, name="ones")
        nc.vector.memset(ones[:], 1.0)
        expo = keep.tile([P, P], F32, name="expo")
        nc.vector.memset(expo[:], 0.0)
        half_max = keep.tile([P, 2 * BLOCKS], F32, name="half_max")

        raw = {}
        grouped = {}
        codes = {}
        scales = {}
        for kind in ("e", "w"):
            for half in range(2):
                key = (kind, half)
                grouped[key] = keep.tile([P, PASSES, HALF, PACK], BF16, name="grouped_%s%d" % key, align_bytes=64)
                codes[key] = keep.tile([P, PASSES, HALF], U32, name="codes_%s%d" % key, align_bytes=64)
                scales[key] = keep.tile([P, PASSES, HALF], U8, name="scales_%s%d" % key, align_bytes=64)
        t_grouped = {}
        t_codes = {}
        t_scales = {}
        for b in range(BLOCKS):
            t_grouped[b] = keep.tile([P, PASSES, P, PACK], BF16, name="t_grouped%d" % b, align_bytes=64)
            t_codes[b] = keep.tile([P, PASSES, P], U32, name="t_codes%d" % b, align_bytes=64)
            t_scales[b] = keep.tile([P, PASSES, P], U8, name="t_scales%d" % b, align_bytes=64)
        t_banks = {}
        c_banks = {}
        early = list(range(CHUNKS))
        late = list(range(CHUNKS, BLOCKS))

        def columns(chunk, count):
            return slice((chunk % CHUNKS) * P, (chunk % CHUNKS + count) * P)

        def load(kind, half, g):
            raw[(kind, half, g)] = keep.tile([P, PACK, HALF], BF16, name="raw_%s%d%d" % (kind, half, g))
            nc.sync.dma_start(
                out=raw[(kind, half, g)][:],
                in_=dram_rows[kind][:, g * PACK:(g + 1) * PACK, half * HALF:(half + 1) * HALF],
            )

        def regroup(engine, kind, g, chunk, count):
            half = chunk // CHUNKS
            src = raw[(kind, half, g)][:, :, columns(chunk, count)].rearrange("p j (c i) -> p c j i", i=4)
            dst = grouped[(kind, half)][:, g, columns(chunk, count), :].rearrange("p (c i) j -> p c j i", i=4)
            if engine == "vector":
                nc.vector.tensor_copy(out=dst, in_=src)
            else:
                nc.scalar.copy(out=dst, in_=src)

        def quantise(kind, g, chunk, count):
            key = (kind, chunk // CHUNKS)
            nc.vector.quantize_mx(
                out=codes[key][:, g, columns(chunk, count)].bitcast(FP8X4),
                scales=scales[key][:, g, columns(chunk, count)],
                in_=grouped[key][:, g, columns(chunk, count), :].rearrange("p n j -> p (n j)"),
            )

        def t_cell(g2, j, b):
            if (g2, b) not in t_banks:
                t_banks[(g2, b)] = psum.tile([P, PACK, P], F32, name="t_bank", tag="bank")
            for g in range(PASSES):
                nc.tensor.matmul_mx(
                    out=t_banks[(g2, b)][:, j, :],
                    lhsT=codes[("w", g2)][:, g, columns(j, 1)].bitcast(FP8X4),
                    lhsT_scale=scales[("w", g2)][:, g, columns(j, 1)],
                    rhs=codes[("e", b // CHUNKS)][:, g, columns(b, 1)].bitcast(FP8X4),
                    rhs_scale=scales[("e", b // CHUNKS)][:, g, columns(b, 1)],
                    start=(g == 0),
                    stop=(g == PASSES - 1),
                )

        def t_cells(g2, chunks, blocks):
            for j in chunks:
                for b in blocks:
                    t_cell(g2, j, b)

        def copy_out_t(g2, b):
            nc.scalar.copy(out=t_grouped[b][:, g2], in_=t_banks[(g2, b)][:].rearrange("p j n -> p n j"))

        def quantise_t(b):
            nc.vector.quantize_mx(
                out=t_codes[b][:].rearrange("p g n -> p (g n)").bitcast(FP8X4),
                scales=t_scales[b][:].rearrange("p g n -> p (g n)"),
                in_=t_grouped[b][:].rearrange("p g n j -> p (g n j)"),
            )

        def c_bank(b, half):
            c_banks[(b, half)] = psum.tile([P, HALF], F32, name="c_bank", tag="bank")
            for g2 in range(PASSES):
                nc.tensor.matmul_mx(
                    out=c_banks[(b, half)][:],
                    lhsT=t_codes[b][:, g2, :].bitcast(FP8X4),
                    lhsT_scale=t_scales[b][:, g2, :],
                    rhs=codes[("e", half)][:, g2, :].bitcast(FP8X4),
                    rhs_scale=scales[("e", half)][:, g2, :],
                    start=(g2 == 0),
                    stop=(g2 == PASSES - 1),
                )

        def row_max(b, half):
            nc.vector.reduce_max(out=half_max[:, 2 * b + half:2 * b + half + 1], in_=c_banks[(b, half)][:], axis=AX.X)

        def keep_clock_up(kind, half, g, count):
            unread = psum.tile([P, HALF], F32, name="unread", tag="bank")
            for i in range(count):
                nc.tensor.matmul(out=unread[:], lhsT=raw[(kind, half, g)][:, 0, 0:P], rhs=raw[(kind, half, g)][:, 1, :],
                                 start=True, stop=True)

        for kind, half in (("e", 0), ("w", 0), ("w", 1), ("e", 1)):
            for g in range(PASSES):
                load(kind, half, g)
        keep_clock_up("e", 0, 1, 4)
        keep_clock_up("w", 0, 0, 4)
        keep_clock_up("w", 0, 1, 2)

        regroup("vector", "e", 0, 0, 2)
        regroup("scalar", "e", 0, 2, 2)
        quantise("e", 0, 0, 2)
        regroup("vector", "e", 1, 0, 2)
        regroup("scalar", "e", 1, 2, 2)
        quantise("e", 0, 2, 2)
        quantise("e", 1, 0, 2)
        left_over = [("e", 1, 2, 2)]
        for half in range(2):
            first = half * CHUNKS
            regroup("vector", "w", 0, first, 2)
            regroup("scalar", "w", 0, first + 2, 2)
            for item in left_over:
                quantise(*item)
            quantise("w", 0, first, 2)
            if half > 0:
                t_cells(half - 1, (2, 3), early)
            regroup("vector", "w", 1, first, 1)
            regroup("vector", "w", 1, first + 1, 1)
            regroup("scalar", "w", 1, first + 2, 1)
            regroup("scalar", "w", 1, first + 3, 1)
            quantise("w", 1, first, 1)
            quantise("w", 0, first + 2, 2)
            quantise("w", 1, first + 1, 1)
            t_cells(half, (0, 1), early)
            left_over = [("w", 1, first + 2, 1), ("w", 1, first + 3, 1)]
        regroup("vector", "e", 0, 4, 2)
        for item in left_over:
            quantise(*item)
        quantise("e", 0, 4, 2)
        t_cells(1, (2, 3), early)
        for b in early:
            copy_out_t(0, b)
        regroup("vector", "e", 1, 4, 2)
        quantise("e", 1, 4, 2)
        regroup("vector", "e", 0, 6, 2)
        regroup("vector", "e", 1, 6, 2)
        copy_out_t(1, 0)
        quantise_t(0)
        quantise("e", 0, 6, 2)
        quantise("e", 1, 6, 2)
        for b in early[1:]:
            copy_out_t(1, b)
            quantise_t(b)

        late_cells = [(g2, j, b) for b in late for g2 in range(PASSES) for j in range(PACK)]
        written = []
        copied = []
        quantised = []

        def next_cells(count, bank_number):
            for g2, j, b in late_cells[len(written):len(written) + count]:
                t_cell(g2, j, b)
                written.append((g2, j, b))
                if j == PACK - 1:
                    copy_out_t(g2, b)
                    if g2 == PASSES - 1:
                        copied.append((b, bank_number))

        next_cells(3 * PACK, -1)
        bank_order = [(b, half) for half in range(2) for b in early] + [(b, half) for b in late for half in range(2)]
        for bank_number, (b, half) in enumerate(bank_order):
            c_bank(b, half)
            next_cells(WEAVE, bank_number)
            for block, since in copied[len(quantised):]:
                if bank_number - since >= LAG:
                    quantise_t(block)
                    quantised.append(block)
            row_max(b, half)

        own_max = keep.tile([P, 1], F32, name="own_max")
        nc.vector.reduce_max(out=own_max[:], in_=half_max[:], axis=AX.X)
        all_max = psum.tile([P, P], F32, name="all_max", tag="bank")
        nc.tensor.transpose(all_max[:], own_max[:, 0:1].to_broadcast([P, P]), ident[:])
        block_max = keep.tile([P, BLOCKS], F32, name="block_max")
        nc.vector.reduce_max(out=block_max[:], in_=half_max[:].rearrange("q (b h) -> q b h", h=2), axis=AX.X)
        tanh_max = keep.tile([P, BLOCKS], F32, name="tanh_max")
        nc.scalar.activation(out=tanh_max[:], in_=block_max[:], func=ACT.Tanh)
        top = keep.tile([P, 1], F32, name="top")
        nc.vector.reduce_max(out=top[:], in_=all_max[:], axis=AX.X)
        minus_top = keep.tile([P, 1], F32, name="minus_top")
        nc.scalar.activation(out=minus_top[:], in_=top[:], func=ACT.Tanh, scale=-1.0)
        row_sum = keep.tile([P, 1], F32, name="row_sum")
        nc.scalar.activation(out=expo[:, 0:BLOCKS], in_=tanh_max[:], func=ACT.Exp, bias=minus_top[:, 0:1], scale=1.0,
                             accum_out=row_sum[:])
        expo_t = psum.tile([P, P], F32, name="expo_t", tag="bank")
        nc.tensor.transpose(expo_t[:], expo[:], ident[:])
        total = psum.tile([P, 1], F32, name="total", tag="bank")
        nc.tensor.matmul(out=total[:], lhsT=ones[:], rhs=row_sum[:], start=True, stop=True)
        inverse = keep.tile([P, 1], F32, name="inverse")
        nc.vector.reciprocal(out=inverse[:], in_=total[:])
        result = keep.tile([P, P], F32, name="result")
        nc.vector.tensor_scalar(out=result[:], in0=expo_t[:], scalar1=inverse[:, 0:1], scalar2=None, op0=ALU.mult)
        nc.sync.dma_start(out=out_rows, in_=result[0:BLOCKS, :])
